import numpy as np
import ml_dtypes


def mxq(x, axis, fmt="e4m3"):
    dtype, down = {"e4m3": (ml_dtypes.float8_e4m3fn, 7), "e5m2": (ml_dtypes.float8_e5m2, 14)}[fmt]
    v = np.moveaxis(np.asarray(x, np.float32).astype(ml_dtypes.bfloat16).astype(np.float64), axis, -1)
    blocks = v.reshape(v.shape[:-1] + (-1, 32))
    amax = np.abs(blocks).max(-1, keepdims=True)
    byte = np.maximum(np.where(amax > 0, np.frexp(amax)[1] - 1 + 127, 0) - down, 1)
    scale = np.exp2(byte - 127.0)
    codes = (blocks / scale).astype(np.float32).astype(dtype).astype(np.float64)
    return np.moveaxis((codes * scale).reshape(v.shape), -1, axis)


WIDE = False


def mx_kscale(k):
    if not WIDE:
        return np.ones(k)
    levels = np.array([10, -10, 5, -5, 0])
    a = np.random.permutation(np.resize(levels, k // 512 * 4)).reshape(k // 512, 4)
    idx = np.arange(k)
    return np.exp2(a[idx // 512, idx % 128 // 32])


BF16 = ml_dtypes.bfloat16


def bf(x):
    return np.asarray(x, np.float32).astype(BF16)


def f64(x):
    return np.asarray(x).astype(np.float64)


B, T, C, A, H = 4, 1024, 512, 1024, 16


def sigmoid(v):
    return 1.0 / (1.0 + np.exp(-v))


def setup_inputs():
    s, t = mx_kscale(C), mx_kscale(A)
    return {"x": bf(np.random.standard_normal((B, T, C)) * s),
            "time_mix": bf(np.random.uniform(0.0, 1.0, (1, 1, C))),
            "Wr": bf(np.random.standard_normal((A, C)) * 1.5 / np.sqrt(C) / s[None, :]),
            "wkv": bf(np.random.standard_normal((B, T, A)) * 1.3 * t),
            "sum_k": bf(np.exp(1.0 + 0.6 * np.random.standard_normal((B, T, A)))),
            "Wo": bf(np.random.standard_normal((C, A)) * 1.5 / np.sqrt(A) / t[None, :])}


def reference(x, time_mix, Wr, wkv, sum_k, Wo):
    x, tm = f64(x), f64(time_mix)
    xs = np.concatenate([np.zeros_like(x[:, :1]), x[:, :-1]], axis=1)
    xm = x * tm + xs * (1.0 - tm)
    r = mxq(xm, 2, "e4m3") @ mxq(f64(Wr), 1, "e4m3").T
    g = sigmoid(r) * f64(wkv) / f64(sum_k)
    return mxq(g, 2, "e4m3") @ mxq(f64(Wo), 1, "e4m3").T

@@ -1,0 +1,351 @@
+from contextlib import ExitStack
+
+import concourse.mybir as mybir
+from concourse.masks import make_identity
+
+FLOPS = 2 * 4096 * 512 * 1024 * 2
+
+BF16 = mybir.dt.bfloat16
+F32 = mybir.dt.float32
+U32 = mybir.dt.uint32
+U8 = mybir.dt.uint8
+FP8X4 = mybir.dt.float8_e4m3fn_x4
+ACT = mybir.ActivationFunctionType
+ALU = mybir.AluOpType
+
+P = 128
+PACK = 4
+K_PASS = P * PACK
+N_SEQ, SEQ_LEN, C_IN, A_DIM = 4, 1024, 512, 1024
+A_PASSES = A_DIM // K_PASS
+A_BLOCKS = A_DIM // P
+N_TILES = N_SEQ * SEQ_LEN // P
+GROUP = 512
+GROUP_TILES = GROUP // P
+CHUNKS = 2
+CHUNK_TILES = N_TILES // CHUNKS
+CHUNK_GROUPS = CHUNK_TILES // GROUP_TILES
+PIECE_ROWS = 2 * P
+AHEAD = 4
+EXP_LEAD = 2
+GATE_LAG = 3
+MIX_LEAD = 8
+QUANT_LEAD = 3
+LATE_TICKS = GATE_LAG + 2
+
+
+def tile_rwkv2timemix_pa_t_kernel(tc, x, time_mix, Wr, wkv, sum_k, Wo, out):
+    nc = tc.nc
+    x_rows = x.flatten_outer_dims()
+    wkv_rows = wkv.flatten_outer_dims()
+    sumk_rows = sum_k.flatten_outer_dims()
+    out_rows = out.flatten_outer_dims()
+
+    with ExitStack() as ctx:
+        keep = ctx.enter_context(tc.tile_pool(name="keep", bufs=1))
+        x_pool = ctx.enter_context(tc.tile_pool(name="x_pool", bufs=CHUNK_GROUPS))
+        planes_pool = ctx.enter_context(tc.tile_pool(name="planes_pool", bufs=2))
+        grouped_pool = ctx.enter_context(tc.tile_pool(name="grouped_pool", bufs=3))
+        xq_pool = ctx.enter_context(tc.tile_pool(name="xq_pool", bufs=CHUNK_GROUPS))
+        sumk_pool = ctx.enter_context(tc.tile_pool(name="sumk_pool", bufs=AHEAD))
+        wkv_pool = ctx.enter_context(tc.tile_pool(name="wkv_pool", bufs=AHEAD + 2))
+        ratio_pool = ctx.enter_context(tc.tile_pool(name="ratio_pool", bufs=CHUNK_TILES + 1))
+        tanh_pool = ctx.enter_context(tc.tile_pool(name="tanh_pool", bufs=8))
+        gate_pool = ctx.enter_context(tc.tile_pool(name="gate_pool", bufs=3))
+        gq_pool = ctx.enter_context(tc.tile_pool(name="gq_pool", bufs=4))
+        o_pool = ctx.enter_context(tc.tile_pool(name="o_pool", bufs=6))
+        psum_wide = ctx.enter_context(tc.psum_pool(name="psum_wide", bufs=4))
+        psum_ratio = ctx.enter_context(tc.psum_pool(name="psum_ratio", bufs=2))
+        psum_out = ctx.enter_context(tc.psum_pool(name="psum_out", bufs=2))
+        ctx.enter_context(tc.manual_schedule())
+
+        sumk_tiles = {}
+        wkv_tiles = {}
+        ratio_tiles = {}
+        x_tiles = {}
+        x_words = {}
+        x_scales = {}
+        tanh_tiles = {}
+        gate_words = {}
+        gate_scales = {}
+        out_banks = {}
+
+        def load_sumk(i):
+            sumk_tiles[i] = sumk_pool.tile([P, A_DIM], BF16, name="sumk_t")
+            nc.sync.dma_start(out=sumk_tiles[i][:], in_=sumk_rows[P * i : P * (i + 1), :])
+
+        def load_wkv(i):
+            wkv_tiles[i] = wkv_pool.tile([P, A_DIM], BF16, name="wkv_t")
+            nc.sync.dma_start(out=wkv_tiles[i][:], in_=wkv_rows[P * i : P * (i + 1), :])
+
+        def load_rows(dst, rows):
+            nc.sync.dma_start(out=dst, in_=rows.rearrange("(n p) w -> p n w", p=P))
+
+        def load_x(g, h):
+            if h == 0:
+                x_tiles[g] = x_pool.tile([P, GROUP_TILES, C_IN], BF16, name="x_t")
+            r0 = GROUP * g + PIECE_ROWS * h
+            load_rows(x_tiles[g][:, 2 * h : 2 * h + 2, :], x_rows[r0 : r0 + PIECE_ROWS, :])
+
+        def x_loads(groups):
+            return [lambda g=g, h=h: load_x(g, h) for g in groups for h in range(2)]
+
+        ident_bf = keep.tile([P, P], BF16, name="ident_bf")
+        make_identity(nc, ident_bf[:])
+        ident_f32 = keep.tile([P, P], F32, name="ident_f32")
+        make_identity(nc, ident_f32[:])
+
+        load_sumk(0)
+        load_x(0, 0)
+        load_x(0, 1)
+
+        mix_rows = keep.tile([P, P], BF16, name="mix_rows")
+        nc.vector.memset(mix_rows[:], 0.0)
+        nc.sync.dma_start(out=mix_rows[0:PACK, :], in_=time_mix.rearrange("a b (j p) -> (a b j) p", p=P))
+        for i in range(1, AHEAD):
+            load_sumk(i)
+        mix_ps = psum_wide.tile([P, P], BF16, name="mix_ps", tag="wide")
+        nc.tensor.transpose(mix_ps[:], mix_rows[:], ident_bf[:])
+        mix_col = keep.tile([P, PACK], F32, name="mix_col")
+        nc.vector.tensor_copy(out=mix_col[:], in_=mix_ps[:, 0:PACK])
+        rest_col = keep.tile([P, PACK], F32, name="rest_col")
+        nc.vector.tensor_scalar(
+            out=rest_col[:], in0=mix_col[:], scalar1=-1.0, scalar2=1.0, op0=ALU.mult, op1=ALU.add
+        )
+
+        carry = keep.tile([P, PACK, SEQ_LEN], F32, name="carry")
+        nc.vector.memset(carry[:, :, 0:1], 0.0)
+
+        wr_words = keep.tile([P, A_DIM], U32, name="wr_words", align_bytes=64)
+        wr_scales = keep.tile([P, A_DIM], U8, name="wr_scales", align_bytes=64)
+        wo_words = keep.tile([P, A_PASSES, C_IN], U32, name="wo_words", align_bytes=64)
+        wo_scales = keep.tile([P, A_PASSES, C_IN], U8, name="wo_scales", align_bytes=64)
+
+        def mix_group(g):
+            t0 = GROUP * g % SEQ_LEN
+            banks = []
+            for pair in range(PACK // 2):
+                x_ps = psum_wide.tile([P, 2, GROUP], BF16, name="x_ps", tag="wide")
+                for h in range(2):
+                    j = 2 * pair + h
+                    for n in range(GROUP_TILES):
+                        nc.tensor.transpose(
+                            x_ps[:, h, P * n : P * (n + 1)], x_tiles[g][:, n, P * j : P * (j + 1)], ident_bf[:]
+                        )
+                for h in range(2):
+                    j = 2 * pair + h
+                    width = min(GROUP, SEQ_LEN - 1 - t0)
+                    nc.vector.tensor_scalar_mul(
+                        out=carry[:, j, t0 + 1 : t0 + 1 + width],
+                        in0=x_ps[:, h, 0:width],
+                        scalar1=rest_col[:, j : j + 1],
+                    )
+                banks.append(x_ps)
+            planes = planes_pool.tile([P, PACK, GROUP], BF16, name="planes")
+            for j in range(PACK):
+                nc.vector.scalar_tensor_tensor(
+                    out=planes[:, j, :],
+                    in0=banks[j // 2][:, j % 2, :],
+                    scalar=mix_col[:, j : j + 1],
+                    in1=carry[:, j, t0 : t0 + GROUP],
+                    op0=ALU.mult,
+                    op1=ALU.add,
+                )
+            grouped = grouped_pool.tile([P, GROUP, PACK], BF16, name="grouped", align_bytes=64)
+            nc.gpsimd.tensor_scalar(
+                out=grouped[:],
+                in0=planes[:].rearrange("p j t -> p t j"),
+                scalar1=1.0,
+                scalar2=0.0,
+                op0=ALU.mult,
+                op1=ALU.add,
+            )
+            return grouped
+
+        def quantise_group(g, grouped):
+            x_words[g] = xq_pool.tile([P, GROUP], U32, name="x_words_t", align_bytes=64)
+            x_scales[g] = xq_pool.tile([P, GROUP], U8, name="x_scales_t", align_bytes=64)
+            nc.vector.quantize_mx(
+                out=x_words[g][:].bitcast(FP8X4),
+                scales=x_scales[g][:],
+                in_=grouped[:].rearrange("p t j -> p (t j)"),
+            )
+
+        def weight_loads(w, row_tiles, width):
+            half_tiles = row_tiles // 2
+            step = PIECE_ROWS * C_IN // width // P
+            halves = []
+            loads = []
+            for h in range(2):
+                w_t = tanh_pool.tile([P, half_tiles, width], BF16, name="w_t", tag="tanh")
+                halves.append(w_t)
+                for s in range(0, half_tiles, step):
+                    r0 = P * (half_tiles * h + s)
+                    loads.append(lambda dst=w_t[:, s : s + step, :], rows=w[r0 : r0 + P * step, :]: load_rows(dst, rows))
+            return halves, loads
+
+        def quantise_weight(halves, row_tiles, passes, words, scales):
+            units = [(c, m) for c in range(passes) for m in range(row_tiles)]
+            grouped = grouped_pool.tile([P, len(units) * P, PACK], BF16, name="w_grouped", bufs=1, align_bytes=64)
+            for pair in range(len(units) // 2):
+                w_ps = psum_wide.tile([P, 2, PACK, P], BF16, name="w_ps", tag="wide")
+                for h in range(2):
+                    c, m = units[2 * pair + h]
+                    w_t = halves[m // (row_tiles // 2)]
+                    for j in range(PACK):
+                        k0 = K_PASS * c + P * j
+                        nc.tensor.transpose(w_ps[:, h, j, :], w_t[:, m % (row_tiles // 2), k0 : k0 + P], ident_bf[:])
+                nc.vector.tensor_copy(
+                    out=grouped[:, 2 * P * pair : 2 * P * (pair + 1), :].rearrange("p (h r) j -> p h r j", h=2),
+                    in_=w_ps[:].rearrange("p h j r -> p h r j"),
+                )
+            nc.vector.quantize_mx(
+                out=words.bitcast(FP8X4), scales=scales, in_=grouped[:].rearrange("p r j -> p (r j)")
+            )
+
+        def ln_sumk(i):
+            ratio_tiles[i] = ratio_pool.tile([P, A_DIM], F32, name="ratio_t")
+            nc.scalar.activation(out=ratio_tiles[i][:], in_=sumk_tiles[i][:], func=ACT.Ln, scale=2.0)
+
+        def exp_and_ratio(i):
+            nc.scalar.activation(out=ratio_tiles[i][:], in_=ratio_tiles[i][:], func=ACT.Exp, scale=-1.0)
+            nc.gpsimd.tensor_tensor(out=ratio_tiles[i][:], in0=wkv_tiles[i][:], in1=ratio_tiles[i][:], op=ALU.mult)
+
+        def receptance(i):
+            g = i // GROUP_TILES
+            t0 = P * (i % GROUP_TILES)
+            tanh_tiles[i] = tanh_pool.tile([P, A_BLOCKS, P], F32, name="tanh_t", tag="tanh")
+            for c in range(A_PASSES):
+                r_ps = psum_wide.tile([P, PACK, P], F32, name="r_ps", tag="wide")
+                for j in range(PACK):
+                    a0 = K_PASS * c + P * j
+                    nc.tensor.matmul_mx(
+                        out=r_ps[:, j, :],
+                        lhsT=wr_words[:, a0 : a0 + P].bitcast(FP8X4),
+                        lhsT_scale=wr_scales[:, a0 : a0 + P],
+                        rhs=x_words[g][:, t0 : t0 + P].bitcast(FP8X4),
+                        rhs_scale=x_scales[g][:, t0 : t0 + P],
+                        start=True,
+                        stop=True,
+                    )
+                nc.scalar.activation(
+                    out=tanh_tiles[i][:, PACK * c : PACK * (c + 1), :], in_=r_ps[:], func=ACT.Tanh, scale=0.5
+                )
+
+        def gate(i):
+            gate_t = gate_pool.tile([P, A_PASSES, P, PACK], BF16, name="gate_t", align_bytes=64)
+            for c in range(A_PASSES):
+                ratio_ps = psum_ratio.tile([P, PACK, P], F32, name="ratio_ps")
+                for j in range(PACK):
+                    a0 = K_PASS * c + P * j
+                    nc.tensor.transpose(ratio_ps[:, j, :], ratio_tiles[i][:, a0 : a0 + P], ident_f32[:])
+                nc.vector.scalar_tensor_tensor(
+                    out=gate_t[:, c, :, :],
+                    in0=tanh_tiles[i][:, PACK * c : PACK * (c + 1), :].rearrange("p j t -> p t j"),
+                    scalar=1.0,
+                    in1=ratio_ps[:].rearrange("p j t -> p t j"),
+                    op0=ALU.add,
+                    op1=ALU.mult,
+                )
+            return gate_t
+
+        def quantise_gate(i, gate_t):
+            gate_words[i] = gq_pool.tile([P, A_PASSES, P], U32, name="gate_words_t", align_bytes=64)
+            gate_scales[i] = gq_pool.tile([P, A_PASSES, P], U8, name="gate_scales_t", align_bytes=64)
+            nc.vector.quantize_mx(
+                out=gate_words[i][:].rearrange("p c t -> p (c t)").bitcast(FP8X4),
+                scales=gate_scales[i][:].rearrange("p c t -> p (c t)"),
+                in_=gate_t[:].rearrange("p c t j -> p (c t j)"),
+            )
+
+        def project(i):
+            out_banks[i] = psum_out.tile([P, C_IN], F32, name="o_ps")
+            for c in range(A_PASSES):
+                nc.tensor.matmul_mx(
+                    out=out_banks[i][:],
+                    lhsT=gate_words[i][:, c, :].bitcast(FP8X4),
+                    lhsT_scale=gate_scales[i][:, c, :],
+                    rhs=wo_words[:, c, :].bitcast(FP8X4),
+                    rhs_scale=wo_scales[:, c, :],
+                    start=(c == 0),
+                    stop=(c == A_PASSES - 1),
+                )
+
+        def store(i):
+            o_sb = o_pool.tile([P, C_IN], F32, name="o_sb")
+            nc.vector.tensor_copy(out=o_sb[:], in_=out_banks[i][:])
+            nc.sync.dma_start(out=out_rows[P * i : P * (i + 1), :], in_=o_sb[:])
+
+        def tick(chunk, t):
+            first = chunk * CHUNK_TILES
+
+            def tile_at(lag):
+                return first + t - lag if 0 <= t - lag < CHUNK_TILES else None
+
+            i_exp = tile_at(0)
+            i_tanh = tile_at(EXP_LEAD)
+            i_gate = tile_at(EXP_LEAD + GATE_LAG)
+            i_proj = tile_at(EXP_LEAD + GATE_LAG + 1)
+            i_store = tile_at(EXP_LEAD + GATE_LAG + 2)
+            if i_gate is not None:
+                gate_t = gate(i_gate)
+            if i_store is not None:
+                store(i_store)
+            if i_gate is not None:
+                quantise_gate(i_gate, gate_t)
+            if i_proj is not None:
+                project(i_proj)
+            if i_exp is not None:
+                exp_and_ratio(i_exp)
+                if t + AHEAD < CHUNK_TILES:
+                    load_wkv(i_exp + AHEAD)
+            if i_tanh is not None:
+                receptance(i_tanh)
+
+        wr_halves, wr_loads = weight_loads(Wr, A_DIM // P, C_IN)
+        wo_halves, wo_loads = weight_loads(Wo, C_IN // P, A_DIM)
+        side_loads = wr_loads + x_loads([1]) + wo_loads + x_loads(range(2, CHUNK_GROUPS))
+        for chunk in range(CHUNKS):
+            for n in range(CHUNK_TILES):
+                i = chunk * CHUNK_TILES + n
+                ln_sumk(i)
+                if n + AHEAD < CHUNK_TILES:
+                    load_sumk(i + AHEAD)
+                else:
+                    load_wkv(i + AHEAD - CHUNK_TILES)
+                if n < len(side_loads):
+                    side_loads[n]()
+                if chunk > 0 and n % 2 == 1 and n // 2 < LATE_TICKS:
+                    tick(chunk - 1, CHUNK_TILES + EXP_LEAD + n // 2)
+
+            first_group = chunk * CHUNK_GROUPS
+            side_loads = []
+            if chunk + 1 < CHUNKS:
+                for n in range(AHEAD):
+                    load_sumk((chunk + 1) * CHUNK_TILES + n)
+                side_loads = x_loads(range(first_group + CHUNK_GROUPS, first_group + 2 * CHUNK_GROUPS))
+            grouped = {}
+            for t in range(EXP_LEAD - MIX_LEAD, CHUNK_TILES + EXP_LEAD):
+                if t >= 0:
+                    tick(chunk, t)
+                for k in range(CHUNK_GROUPS):
+                    first_use = GROUP_TILES * k + EXP_LEAD
+                    if t == first_use - MIX_LEAD:
+                        grouped[k] = mix_group(first_group + k)
+                        if chunk == 0 and k == 0:
+                            quantise_weight(wr_halves, A_DIM // P, 1, wr_words[:], wr_scales[:])
+                        if chunk == 0 and k == 1:
+                            quantise_weight(
+                                wo_halves,
+                                C_IN // P,
+                                A_PASSES,
+                                wo_words[:].rearrange("p c r -> p (c r)"),
+                                wo_scales[:].rearrange("p c r -> p (c r)"),
+                            )
+                    if t == first_use - QUANT_LEAD:
+                        quantise_group(first_group + k, grouped[k])
+                if 0 <= t < len(side_loads):
+                    side_loads[t]()
+            side_loads = []
+        for t in range(LATE_TICKS):
+            tick(CHUNKS - 1, CHUNK_TILES + EXP_LEAD + t)

@@ -27,6 +27,7 @@ CHUNK_TILES = N_TILES // CHUNKS
 CHUNK_GROUPS = CHUNK_TILES // GROUP_TILES
 PIECE_ROWS = 2 * P
 AHEAD = 4
+SUMK_AHEAD = 8
 EXP_LEAD = 2
 GATE_LAG = 3
 MIX_LEAD = 8
@@ -47,7 +48,7 @@ def tile_rwkv2timemix_pa_t_kernel(tc, x, time_mix, Wr, wkv, sum_k, Wo, out):
         planes_pool = ctx.enter_context(tc.tile_pool(name="planes_pool", bufs=2))
         grouped_pool = ctx.enter_context(tc.tile_pool(name="grouped_pool", bufs=3))
         xq_pool = ctx.enter_context(tc.tile_pool(name="xq_pool", bufs=CHUNK_GROUPS))
-        sumk_pool = ctx.enter_context(tc.tile_pool(name="sumk_pool", bufs=AHEAD))
+        sumk_pool = ctx.enter_context(tc.tile_pool(name="sumk_pool", bufs=SUMK_AHEAD))
         wkv_pool = ctx.enter_context(tc.tile_pool(name="wkv_pool", bufs=AHEAD + 2))
         ratio_pool = ctx.enter_context(tc.tile_pool(name="ratio_pool", bufs=CHUNK_TILES + 1))
         tanh_pool = ctx.enter_context(tc.tile_pool(name="tanh_pool", bufs=8))
@@ -102,7 +103,7 @@ def tile_rwkv2timemix_pa_t_kernel(tc, x, time_mix, Wr, wkv, sum_k, Wo, out):
         mix_rows = keep.tile([P, P], BF16, name="mix_rows")
         nc.vector.memset(mix_rows[:], 0.0)
         nc.sync.dma_start(out=mix_rows[0:PACK, :], in_=time_mix.rearrange("a b (j p) -> (a b j) p", p=P))
-        for i in range(1, AHEAD):
+        for i in range(1, SUMK_AHEAD):
             load_sumk(i)
         mix_ps = psum_wide.tile([P, P], BF16, name="mix_ps", tag="wide")
         nc.tensor.transpose(mix_ps[:], mix_rows[:], ident_bf[:])
@@ -309,9 +310,9 @@ def tile_rwkv2timemix_pa_t_kernel(tc, x, time_mix, Wr, wkv, sum_k, Wo, out):
             for n in range(CHUNK_TILES):
                 i = chunk * CHUNK_TILES + n
                 ln_sumk(i)
-                if n + AHEAD < CHUNK_TILES:
-                    load_sumk(i + AHEAD)
-                else:
+                if n + SUMK_AHEAD < CHUNK_TILES:
+                    load_sumk(i + SUMK_AHEAD)
+                if n + AHEAD >= CHUNK_TILES:
                     load_wkv(i + AHEAD - CHUNK_TILES)
                 if n < len(side_loads):
                     side_loads[n]()
@@ -321,7 +322,7 @@ def tile_rwkv2timemix_pa_t_kernel(tc, x, time_mix, Wr, wkv, sum_k, Wo, out):
             first_group = chunk * CHUNK_GROUPS
             side_loads = []
             if chunk + 1 < CHUNKS:
-                for n in range(AHEAD):
+                for n in range(SUMK_AHEAD):
                     load_sumk((chunk + 1) * CHUNK_TILES + n)
                 side_loads = x_loads(range(first_group + CHUNK_GROUPS, first_group + 2 * CHUNK_GROUPS))
             grouped = {}

@@ -22,17 +22,31 @@ A_BLOCKS = A_DIM // P
 N_TILES = N_SEQ * SEQ_LEN // P
 GROUP = 512
 GROUP_TILES = GROUP // P
-CHUNKS = 2
-CHUNK_TILES = N_TILES // CHUNKS
-CHUNK_GROUPS = CHUNK_TILES // GROUP_TILES
-PIECE_ROWS = 2 * P
-AHEAD = 4
-SUMK_AHEAD = 8
-EXP_LEAD = 2
-GATE_LAG = 3
-MIX_LEAD = 8
-QUANT_LEAD = 3
-LATE_TICKS = GATE_LAG + 2
+N_GROUPS = N_TILES // GROUP_TILES
+PAD = 2
+SUMK_AHEAD = 5
+W_AHEAD = 6
+IN_BUFS = 7
+BIG = 7
+OB = 4
+PA = 2
+PR = 4
+PO = 2
+SQ0 = 4
+A1 = 10
+W_LEAD = 2
+W_EARLY = 4
+PREP_T = 30
+R0_AT = 25
+MGROUPS = (1, 3, 4, 5, 6, 7)
+E_LAG = 2
+SQ_T2 = 30
+D_LAG = 1
+Q_LAG = 2
+S_LAST = 28
+QUANTS = [4] * 7 + [2, 2]
+QUANT_OF = [(k, h) for k in range(len(QUANTS)) for h in range(QUANTS[k])]
+QUANT_END = [sum(QUANTS[: k + 1]) for k in range(len(QUANTS))]
 
 
 def tile_rwkv2timemix_pa_t_kernel(tc, x, time_mix, Wr, wkv, sum_k, Wo, out):
@@ -44,52 +58,38 @@ def tile_rwkv2timemix_pa_t_kernel(tc, x, time_mix, Wr, wkv, sum_k, Wo, out):
 
     with ExitStack() as ctx:
         keep = ctx.enter_context(tc.tile_pool(name="keep", bufs=1))
-        x_pool = ctx.enter_context(tc.tile_pool(name="x_pool", bufs=CHUNK_GROUPS))
-        planes_pool = ctx.enter_context(tc.tile_pool(name="planes_pool", bufs=2))
-        grouped_pool = ctx.enter_context(tc.tile_pool(name="grouped_pool", bufs=3))
-        xq_pool = ctx.enter_context(tc.tile_pool(name="xq_pool", bufs=CHUNK_GROUPS))
-        sumk_pool = ctx.enter_context(tc.tile_pool(name="sumk_pool", bufs=SUMK_AHEAD))
-        wkv_pool = ctx.enter_context(tc.tile_pool(name="wkv_pool", bufs=AHEAD + 2))
-        ratio_pool = ctx.enter_context(tc.tile_pool(name="ratio_pool", bufs=CHUNK_TILES + 1))
-        tanh_pool = ctx.enter_context(tc.tile_pool(name="tanh_pool", bufs=8))
-        gate_pool = ctx.enter_context(tc.tile_pool(name="gate_pool", bufs=3))
-        gq_pool = ctx.enter_context(tc.tile_pool(name="gq_pool", bufs=4))
-        o_pool = ctx.enter_context(tc.tile_pool(name="o_pool", bufs=6))
-        psum_wide = ctx.enter_context(tc.psum_pool(name="psum_wide", bufs=4))
-        psum_ratio = ctx.enter_context(tc.psum_pool(name="psum_ratio", bufs=2))
-        psum_out = ctx.enter_context(tc.psum_pool(name="psum_out", bufs=2))
+        big_pool = ctx.enter_context(tc.tile_pool(name="big_pool", bufs=BIG))
+        xq_pool = ctx.enter_context(tc.tile_pool(name="xq_pool", bufs=N_GROUPS))
+        in_pool = ctx.enter_context(tc.tile_pool(name="in_pool", bufs=IN_BUFS))
+        ratio_pool = ctx.enter_context(tc.tile_pool(name="ratio_pool", bufs=N_TILES))
+        gate_pool = ctx.enter_context(tc.tile_pool(name="gate_pool", bufs=2))
+        gq_pool = ctx.enter_context(tc.tile_pool(name="gq_pool", bufs=2))
+        o_pool = ctx.enter_context(tc.tile_pool(name="o_pool", bufs=OB))
+        psum_r = ctx.enter_context(tc.psum_pool(name="psum_r", bufs=PA))
+        psum_turn = ctx.enter_context(tc.psum_pool(name="psum_turn", bufs=PR))
+        psum_out = ctx.enter_context(tc.psum_pool(name="psum_out", bufs=PO))
         ctx.enter_context(tc.manual_schedule())
 
-        sumk_tiles = {}
-        wkv_tiles = {}
-        ratio_tiles = {}
-        x_tiles = {}
-        x_words = {}
-        x_scales = {}
-        tanh_tiles = {}
-        gate_words = {}
-        gate_scales = {}
-        out_banks = {}
+        sumk_tiles, wkv_tiles, ratio_tiles, x_tiles, xts, grouped = {}, {}, {}, {}, {}, {}
+        x_words, x_scales, tanh_tiles, r_banks, ratio_banks = {}, {}, {}, {}, {}
+        gate_tiles, gate_words, gate_scales, out_banks = {}, {}, {}, {}
 
         def load_sumk(i):
-            sumk_tiles[i] = sumk_pool.tile([P, A_DIM], BF16, name="sumk_t")
+            sumk_tiles[i] = in_pool.tile([P, A_DIM], BF16, name="sumk_t", tag="in")
             nc.sync.dma_start(out=sumk_tiles[i][:], in_=sumk_rows[P * i : P * (i + 1), :])
 
         def load_wkv(i):
-            wkv_tiles[i] = wkv_pool.tile([P, A_DIM], BF16, name="wkv_t")
+            wkv_tiles[i] = in_pool.tile([P, A_DIM], BF16, name="wkv_t", tag="in")
             nc.sync.dma_start(out=wkv_tiles[i][:], in_=wkv_rows[P * i : P * (i + 1), :])
 
         def load_rows(dst, rows):
             nc.sync.dma_start(out=dst, in_=rows.rearrange("(n p) w -> p n w", p=P))
 
-        def load_x(g, h):
-            if h == 0:
-                x_tiles[g] = x_pool.tile([P, GROUP_TILES, C_IN], BF16, name="x_t")
-            r0 = GROUP * g + PIECE_ROWS * h
-            load_rows(x_tiles[g][:, 2 * h : 2 * h + 2, :], x_rows[r0 : r0 + PIECE_ROWS, :])
-
-        def x_loads(groups):
-            return [lambda g=g, h=h: load_x(g, h) for g in groups for h in range(2)]
+        def load_x(g):
+            x_tiles[g] = big_pool.tile([P, GROUP_TILES, C_IN], BF16, name="x_t", tag="big", align_bytes=64)
+            for h in range(2):
+                r0 = GROUP * g + 2 * P * h
+                load_rows(x_tiles[g][:, 2 * h : 2 * h + 2, :], x_rows[r0 : r0 + 2 * P, :])
 
         ident_bf = keep.tile([P, P], BF16, name="ident_bf")
         make_identity(nc, ident_bf[:])
@@ -97,15 +97,13 @@ def tile_rwkv2timemix_pa_t_kernel(tc, x, time_mix, Wr, wkv, sum_k, Wo, out):
         make_identity(nc, ident_f32[:])
 
         load_sumk(0)
-        load_x(0, 0)
-        load_x(0, 1)
-
+        load_x(0)
         mix_rows = keep.tile([P, P], BF16, name="mix_rows")
         nc.vector.memset(mix_rows[:], 0.0)
         nc.sync.dma_start(out=mix_rows[0:PACK, :], in_=time_mix.rearrange("a b (j p) -> (a b j) p", p=P))
         for i in range(1, SUMK_AHEAD):
             load_sumk(i)
-        mix_ps = psum_wide.tile([P, P], BF16, name="mix_ps", tag="wide")
+        mix_ps = psum_out.tile([P, P], BF16, name="mix_ps", tag="o_ps")
         nc.tensor.transpose(mix_ps[:], mix_rows[:], ident_bf[:])
         mix_col = keep.tile([P, PACK], F32, name="mix_col")
         nc.vector.tensor_copy(out=mix_col[:], in_=mix_ps[:, 0:PACK])
@@ -113,83 +111,153 @@ def tile_rwkv2timemix_pa_t_kernel(tc, x, time_mix, Wr, wkv, sum_k, Wo, out):
         nc.vector.tensor_scalar(
             out=rest_col[:], in0=mix_col[:], scalar1=-1.0, scalar2=1.0, op0=ALU.mult, op1=ALU.add
         )
-
-        carry = keep.tile([P, PACK, SEQ_LEN], F32, name="carry")
-        nc.vector.memset(carry[:, :, 0:1], 0.0)
+        diags = keep.tile([P, 2, PACK, P], BF16, name="diags")
+        for j in range(PACK):
+            for h in range(2):
+                nc.vector.tensor_scalar(
+                    out=diags[:, h, j, :],
+                    in0=ident_bf[:],
+                    scalar1=mix_col[:, j : j + 1],
+                    scalar2=1.0 - 2.0 * h,
+                    op0=ALU.mult,
+                    op1=ALU.mult,
+                )
 
         wr_words = keep.tile([P, A_DIM], U32, name="wr_words", align_bytes=64)
         wr_scales = keep.tile([P, A_DIM], U8, name="wr_scales", align_bytes=64)
         wo_words = keep.tile([P, A_PASSES, C_IN], U32, name="wo_words", align_bytes=64)
         wo_scales = keep.tile([P, A_PASSES, C_IN], U8, name="wo_scales", align_bytes=64)
 
-        def mix_group(g):
-            t0 = GROUP * g % SEQ_LEN
-            banks = []
-            for pair in range(PACK // 2):
-                x_ps = psum_wide.tile([P, 2, GROUP], BF16, name="x_ps", tag="wide")
+        def new_xt(g):
+            xts[g] = big_pool.tile([P, PACK, GROUP + PAD], BF16, name="xt", tag="big", align_bytes=64)
+
+        def turn_x(g, pair):
+            x_ps = psum_turn.tile([P, 2, GROUP], BF16, name="x_ps", tag="turn")
+            for h in range(2):
+                j = 2 * pair + h
+                for n in range(GROUP_TILES):
+                    nc.tensor.transpose(
+                        x_ps[:, h, P * n : P * (n + 1)], x_tiles[g][:, n, P * j : P * (j + 1)], ident_bf[:]
+                    )
+            return x_ps
+
+        def carry_last(g, pair, x_ps):
+            if g % 2 == 0:
+                nc.vector.tensor_copy(
+                    out=xts[g + 1][:, 2 * pair : 2 * pair + 2, 0:PAD], in_=x_ps[:, :, GROUP - PAD : GROUP]
+                )
+
+        def x_turn(g):
+            if g % 2 == 0:
+                new_xt(g)
+                nc.vector.memset(xts[g][:, :, 0:PAD], 0.0)
+                new_xt(g + 1)
+            for pair in range(2):
+                x_ps = turn_x(g, pair)
+                nc.vector.tensor_copy(out=xts[g][:, 2 * pair : 2 * pair + 2, PAD : PAD + GROUP], in_=x_ps[:])
+                carry_last(g, pair, x_ps)
+
+        def x_mix(g, n):
+            if n == 0:
+                grouped[g] = big_pool.tile([P, GROUP, PACK], BF16, name="grouped_t", tag="big", align_bytes=64)
+            now = xts[g][:, :, PAD + P * n : PAD + P * (n + 1)]
+            before = xts[g][:, :, PAD - 1 + P * n : PAD - 1 + P * (n + 1)]
+            m_ps = psum_out.tile([P, PACK, P], F32, name="m_ps", tag="o_ps")
+            for j in range(PACK):
+                nc.tensor.matmul(m_ps[:, j, :], lhsT=diags[:, 0, j, :], rhs=now[:, j, :], start=True, stop=False)
+                nc.tensor.matmul(m_ps[:, j, :], lhsT=diags[:, 1, j, :], rhs=before[:, j, :], start=False, stop=True)
+            nc.vector.tensor_tensor(
+                out=grouped[g][:, P * n : P * (n + 1), :],
+                in0=m_ps[:].rearrange("p j t -> p t j"),
+                in1=before.rearrange("p j t -> p t j"),
+                op=ALU.add,
+            )
+
+        def direct_jobs(g):
+            held = {}
+
+            def carry(pair):
+                if pair == 0:
+                    new_xt(g + 1)
+                    held["planes"] = big_pool.tile([P, PACK, GROUP], BF16, name="planes", tag="big", align_bytes=64)
+                    held["carry"] = gate_pool.tile([P, PACK, GROUP], F32, name="carry", tag="gate", align_bytes=64)
+                    nc.vector.memset(held["carry"][:, :, 0:1], 0.0)
+                held[pair] = turn_x(g, pair)
                 for h in range(2):
                     j = 2 * pair + h
-                    for n in range(GROUP_TILES):
-                        nc.tensor.transpose(
-                            x_ps[:, h, P * n : P * (n + 1)], x_tiles[g][:, n, P * j : P * (j + 1)], ident_bf[:]
-                        )
-                for h in range(2):
-                    j = 2 * pair + h
-                    width = min(GROUP, SEQ_LEN - 1 - t0)
                     nc.vector.tensor_scalar_mul(
-                        out=carry[:, j, t0 + 1 : t0 + 1 + width],
-                        in0=x_ps[:, h, 0:width],
+                        out=held["carry"][:, j, 1:GROUP],
+                        in0=held[pair][:, h, 0 : GROUP - 1],
                         scalar1=rest_col[:, j : j + 1],
                     )
-                banks.append(x_ps)
-            planes = planes_pool.tile([P, PACK, GROUP], BF16, name="planes")
-            for j in range(PACK):
-                nc.vector.scalar_tensor_tensor(
-                    out=planes[:, j, :],
-                    in0=banks[j // 2][:, j % 2, :],
-                    scalar=mix_col[:, j : j + 1],
-                    in1=carry[:, j, t0 : t0 + GROUP],
-                    op0=ALU.mult,
-                    op1=ALU.add,
-                )
-            grouped = grouped_pool.tile([P, GROUP, PACK], BF16, name="grouped", align_bytes=64)
-            nc.gpsimd.tensor_scalar(
-                out=grouped[:],
-                in0=planes[:].rearrange("p j t -> p t j"),
-                scalar1=1.0,
-                scalar2=0.0,
-                op0=ALU.mult,
-                op1=ALU.add,
-            )
-            return grouped
+                carry_last(g, pair, held[pair])
 
-        def quantise_group(g, grouped):
+            def mix(pair):
+                for h in range(2):
+                    j = 2 * pair + h
+                    nc.vector.scalar_tensor_tensor(
+                        out=held["planes"][:, j, :],
+                        in0=held[pair][:, h, :],
+                        scalar=mix_col[:, j : j + 1],
+                        in1=held["carry"][:, j, :],
+                        op0=ALU.mult,
+                        op1=ALU.add,
+                    )
+
+            def interleave():
+                grouped[g] = big_pool.tile([P, GROUP, PACK], BF16, name="grouped_t", tag="big", align_bytes=64)
+                planes = held["planes"][:].rearrange("p j t -> p t j")
+                if g == 0:
+                    nc.gpsimd.tensor_scalar(
+                        out=grouped[g][:], in0=planes, scalar1=1.0, scalar2=0.0, op0=ALU.mult, op1=ALU.add
+                    )
+                else:
+                    nc.vector.tensor_copy(out=grouped[g][:], in_=planes)
+
+            return [lambda: carry(0), lambda: mix(0), lambda: carry(1), lambda: mix(1), interleave, lambda: x_quant(g)]
+
+        def x_quant(g):
             x_words[g] = xq_pool.tile([P, GROUP], U32, name="x_words_t", align_bytes=64)
             x_scales[g] = xq_pool.tile([P, GROUP], U8, name="x_scales_t", align_bytes=64)
             nc.vector.quantize_mx(
                 out=x_words[g][:].bitcast(FP8X4),
                 scales=x_scales[g][:],
-                in_=grouped[:].rearrange("p t j -> p (t j)"),
+                in_=grouped[g][:].rearrange("p t j -> p (t j)"),
             )
+
+        def x_jobs(g):
+            if g in MGROUPS:
+                return (
+                    [lambda: x_turn(g)] + [lambda n=n: x_mix(g, n) for n in range(GROUP_TILES)] + [lambda: x_quant(g)]
+                )
+            return direct_jobs(g)
 
         def weight_loads(w, row_tiles, width):
             half_tiles = row_tiles // 2
-            step = PIECE_ROWS * C_IN // width // P
+            step = 2 * P * C_IN // width // P
             halves = []
             loads = []
             for h in range(2):
-                w_t = tanh_pool.tile([P, half_tiles, width], BF16, name="w_t", tag="tanh")
+                w_t = ratio_pool.tile([P, half_tiles, width], BF16, name="w_t", tag="ratio")
                 halves.append(w_t)
                 for s in range(0, half_tiles, step):
                     r0 = P * (half_tiles * h + s)
-                    loads.append(lambda dst=w_t[:, s : s + step, :], rows=w[r0 : r0 + P * step, :]: load_rows(dst, rows))
+                    loads.append(
+                        lambda dst=w_t[:, s : s + step, :], rows=w[r0 : r0 + P * step, :]: load_rows(dst, rows)
+                    )
             return halves, loads
 
-        def quantise_weight(halves, row_tiles, passes, words, scales):
+        def weight_jobs(halves, row_tiles, passes, words, scales):
             units = [(c, m) for c in range(passes) for m in range(row_tiles)]
-            grouped = grouped_pool.tile([P, len(units) * P, PACK], BF16, name="w_grouped", bufs=1, align_bytes=64)
-            for pair in range(len(units) // 2):
-                w_ps = psum_wide.tile([P, 2, PACK, P], BF16, name="w_ps", tag="wide")
+            held = []
+
+            def turn(pair):
+                if pair == 0:
+                    held.append(
+                        gate_pool.tile([P, len(units) * P, PACK], BF16, name="grouped_w", tag="gate", align_bytes=64)
+                    )
+                grouped_w = held[0]
+                w_ps = psum_turn.tile([P, 2, PACK, P], BF16, name="w_ps", tag="turn")
                 for h in range(2):
                     c, m = units[2 * pair + h]
                     w_t = halves[m // (row_tiles // 2)]
@@ -197,31 +265,40 @@ def tile_rwkv2timemix_pa_t_kernel(tc, x, time_mix, Wr, wkv, sum_k, Wo, out):
                         k0 = K_PASS * c + P * j
                         nc.tensor.transpose(w_ps[:, h, j, :], w_t[:, m % (row_tiles // 2), k0 : k0 + P], ident_bf[:])
                 nc.vector.tensor_copy(
-                    out=grouped[:, 2 * P * pair : 2 * P * (pair + 1), :].rearrange("p (h r) j -> p h r j", h=2),
+                    out=grouped_w[:, 2 * P * pair : 2 * P * (pair + 1), :].rearrange("p (h r) j -> p h r j", h=2),
                     in_=w_ps[:].rearrange("p h j r -> p h r j"),
                 )
-            nc.vector.quantize_mx(
-                out=words.bitcast(FP8X4), scales=scales, in_=grouped[:].rearrange("p r j -> p (r j)")
+
+            def quant():
+                nc.vector.quantize_mx(
+                    out=words.bitcast(FP8X4), scales=scales, in_=held[0][:].rearrange("p r j -> p (r j)")
+                )
+
+            return [lambda q=q: turn(q) for q in range(len(units) // 2)] + [quant]
+
+        def root(i):
+            ratio_tiles[i] = ratio_pool.tile([P, A_DIM], F32, name="ratio_t", tag="ratio")
+            nc.scalar.activation(
+                out=ratio_tiles[i][:], in_=sumk_tiles[i][:], func=ACT.Abs_reciprocal_sqrt, scale=2.0
             )
 
-        def ln_sumk(i):
-            ratio_tiles[i] = ratio_pool.tile([P, A_DIM], F32, name="ratio_t")
-            nc.scalar.activation(out=ratio_tiles[i][:], in_=sumk_tiles[i][:], func=ACT.Ln, scale=2.0)
+        def square(i):
+            nc.scalar.activation(out=ratio_tiles[i][:], in_=ratio_tiles[i][:], func=ACT.Square)
 
-        def exp_and_ratio(i):
-            nc.scalar.activation(out=ratio_tiles[i][:], in_=ratio_tiles[i][:], func=ACT.Exp, scale=-1.0)
-            nc.gpsimd.tensor_tensor(out=ratio_tiles[i][:], in0=wkv_tiles[i][:], in1=ratio_tiles[i][:], op=ALU.mult)
+        def ratio(i):
+            nc.gpsimd.tensor_tensor(
+                out=ratio_tiles[i][:], in0=wkv_tiles[i][:], in1=ratio_tiles[i][:], op=ALU.mult
+            )
 
         def receptance(i):
             g = i // GROUP_TILES
             t0 = P * (i % GROUP_TILES)
-            tanh_tiles[i] = tanh_pool.tile([P, A_BLOCKS, P], F32, name="tanh_t", tag="tanh")
             for c in range(A_PASSES):
-                r_ps = psum_wide.tile([P, PACK, P], F32, name="r_ps", tag="wide")
+                r_banks[i, c] = psum_r.tile([P, PACK, P], F32, name="r_ps")
                 for j in range(PACK):
                     a0 = K_PASS * c + P * j
                     nc.tensor.matmul_mx(
-                        out=r_ps[:, j, :],
+                        out=r_banks[i, c][:, j, :],
                         lhsT=wr_words[:, a0 : a0 + P].bitcast(FP8X4),
                         lhsT_scale=wr_scales[:, a0 : a0 + P],
                         rhs=x_words[g][:, t0 : t0 + P].bitcast(FP8X4),
@@ -229,43 +306,54 @@ def tile_rwkv2timemix_pa_t_kernel(tc, x, time_mix, Wr, wkv, sum_k, Wo, out):
                         start=True,
                         stop=True,
                     )
+
+        def tanh(i):
+            tanh_tiles[i] = big_pool.tile([P, A_BLOCKS, P], F32, name="tanh_t", tag="big", align_bytes=64)
+            for c in range(A_PASSES):
                 nc.scalar.activation(
-                    out=tanh_tiles[i][:, PACK * c : PACK * (c + 1), :], in_=r_ps[:], func=ACT.Tanh, scale=0.5
+                    out=tanh_tiles[i][:, PACK * c : PACK * (c + 1), :], in_=r_banks[i, c][:], func=ACT.Tanh, scale=0.5
                 )
 
-        def gate(i):
-            gate_t = gate_pool.tile([P, A_PASSES, P, PACK], BF16, name="gate_t", align_bytes=64)
+        def turn_ratio(i):
             for c in range(A_PASSES):
-                ratio_ps = psum_ratio.tile([P, PACK, P], F32, name="ratio_ps")
+                ratio_banks[i, c] = psum_turn.tile([P, PACK, P], F32, name="ratio_ps", tag="turn")
                 for j in range(PACK):
                     a0 = K_PASS * c + P * j
-                    nc.tensor.transpose(ratio_ps[:, j, :], ratio_tiles[i][:, a0 : a0 + P], ident_f32[:])
+                    nc.tensor.transpose(ratio_banks[i, c][:, j, :], ratio_tiles[i][:, a0 : a0 + P], ident_f32[:])
+
+        def gate(i):
+            k, h = QUANT_OF[i]
+            if h == 0:
+                gate_tiles[k] = gate_pool.tile(
+                    [P, QUANTS[k], A_PASSES, P, PACK], BF16, name="gate_t", tag="gate", align_bytes=64
+                )
+            for c in range(A_PASSES):
                 nc.vector.scalar_tensor_tensor(
-                    out=gate_t[:, c, :, :],
+                    out=gate_tiles[k][:, h, c, :, :],
                     in0=tanh_tiles[i][:, PACK * c : PACK * (c + 1), :].rearrange("p j t -> p t j"),
                     scalar=1.0,
-                    in1=ratio_ps[:].rearrange("p j t -> p t j"),
+                    in1=ratio_banks[i, c][:].rearrange("p j t -> p t j"),
                     op0=ALU.add,
                     op1=ALU.mult,
                 )
-            return gate_t
 
-        def quantise_gate(i, gate_t):
-            gate_words[i] = gq_pool.tile([P, A_PASSES, P], U32, name="gate_words_t", align_bytes=64)
-            gate_scales[i] = gq_pool.tile([P, A_PASSES, P], U8, name="gate_scales_t", align_bytes=64)
+        def quantise_gates(k):
+            gate_words[k] = gq_pool.tile([P, QUANTS[k], A_PASSES, P], U32, name="gate_words_t", align_bytes=64)
+            gate_scales[k] = gq_pool.tile([P, QUANTS[k], A_PASSES, P], U8, name="gate_scales_t", align_bytes=64)
             nc.vector.quantize_mx(
-                out=gate_words[i][:].rearrange("p c t -> p (c t)").bitcast(FP8X4),
-                scales=gate_scales[i][:].rearrange("p c t -> p (c t)"),
-                in_=gate_t[:].rearrange("p c t j -> p (c t j)"),
+                out=gate_words[k][:].rearrange("p q c t -> p (q c t)").bitcast(FP8X4),
+                scales=gate_scales[k][:].rearrange("p q c t -> p (q c t)"),
+                in_=gate_tiles[k][:].rearrange("p q c t j -> p (q c t j)"),
             )
 
         def project(i):
-            out_banks[i] = psum_out.tile([P, C_IN], F32, name="o_ps")
+            k, h = QUANT_OF[i]
+            out_banks[i] = psum_out.tile([P, C_IN], F32, name="o_ps", tag="o_ps")
             for c in range(A_PASSES):
                 nc.tensor.matmul_mx(
                     out=out_banks[i][:],
-                    lhsT=gate_words[i][:, c, :].bitcast(FP8X4),
-                    lhsT_scale=gate_scales[i][:, c, :],
+                    lhsT=gate_words[k][:, h, c, :].bitcast(FP8X4),
+                    lhsT_scale=gate_scales[k][:, h, c, :],
                     rhs=wo_words[:, c, :].bitcast(FP8X4),
                     rhs_scale=wo_scales[:, c, :],
                     start=(c == 0),
@@ -274,79 +362,78 @@ def tile_rwkv2timemix_pa_t_kernel(tc, x, time_mix, Wr, wkv, sum_k, Wo, out):
 
         def store(i):
             o_sb = o_pool.tile([P, C_IN], F32, name="o_sb")
-            nc.vector.tensor_copy(out=o_sb[:], in_=out_banks[i][:])
+            if i >= S_LAST:
+                nc.scalar.copy(out=o_sb[:], in_=out_banks[i][:])
+            else:
+                nc.vector.tensor_copy(out=o_sb[:], in_=out_banks[i][:])
             nc.sync.dma_start(out=out_rows[P * i : P * (i + 1), :], in_=o_sb[:])
-
-        def tick(chunk, t):
-            first = chunk * CHUNK_TILES
-
-            def tile_at(lag):
-                return first + t - lag if 0 <= t - lag < CHUNK_TILES else None
-
-            i_exp = tile_at(0)
-            i_tanh = tile_at(EXP_LEAD)
-            i_gate = tile_at(EXP_LEAD + GATE_LAG)
-            i_proj = tile_at(EXP_LEAD + GATE_LAG + 1)
-            i_store = tile_at(EXP_LEAD + GATE_LAG + 2)
-            if i_gate is not None:
-                gate_t = gate(i_gate)
-            if i_store is not None:
-                store(i_store)
-            if i_gate is not None:
-                quantise_gate(i_gate, gate_t)
-            if i_proj is not None:
-                project(i_proj)
-            if i_exp is not None:
-                exp_and_ratio(i_exp)
-                if t + AHEAD < CHUNK_TILES:
-                    load_wkv(i_exp + AHEAD)
-            if i_tanh is not None:
-                receptance(i_tanh)
 
         wr_halves, wr_loads = weight_loads(Wr, A_DIM // P, C_IN)
         wo_halves, wo_loads = weight_loads(Wo, C_IN // P, A_DIM)
-        side_loads = wr_loads + x_loads([1]) + wo_loads + x_loads(range(2, CHUNK_GROUPS))
-        for chunk in range(CHUNKS):
-            for n in range(CHUNK_TILES):
-                i = chunk * CHUNK_TILES + n
-                ln_sumk(i)
-                if n + SUMK_AHEAD < CHUNK_TILES:
-                    load_sumk(i + SUMK_AHEAD)
-                if n + AHEAD >= CHUNK_TILES:
-                    load_wkv(i + AHEAD - CHUNK_TILES)
-                if n < len(side_loads):
-                    side_loads[n]()
-                if chunk > 0 and n % 2 == 1 and n // 2 < LATE_TICKS:
-                    tick(chunk - 1, CHUNK_TILES + EXP_LEAD + n // 2)
+        side_loads = {0: wr_loads[0:1], 1: wr_loads[1:2], 2: wr_loads[2:3], 3: wr_loads[3:4], 6: wo_loads[0:2], 8: wo_loads[2:4]}
+        side_loads[4] = [lambda: load_x(1)]
+        for g in range(2, N_GROUPS):
+            side_loads[4 + 3 * g] = [lambda g=g: load_x(g)]
 
-            first_group = chunk * CHUNK_GROUPS
-            side_loads = []
-            if chunk + 1 < CHUNKS:
-                for n in range(SUMK_AHEAD):
-                    load_sumk((chunk + 1) * CHUNK_TILES + n)
-                side_loads = x_loads(range(first_group + CHUNK_GROUPS, first_group + 2 * CHUNK_GROUPS))
-            grouped = {}
-            for t in range(EXP_LEAD - MIX_LEAD, CHUNK_TILES + EXP_LEAD):
-                if t >= 0:
-                    tick(chunk, t)
-                for k in range(CHUNK_GROUPS):
-                    first_use = GROUP_TILES * k + EXP_LEAD
-                    if t == first_use - MIX_LEAD:
-                        grouped[k] = mix_group(first_group + k)
-                        if chunk == 0 and k == 0:
-                            quantise_weight(wr_halves, A_DIM // P, 1, wr_words[:], wr_scales[:])
-                        if chunk == 0 and k == 1:
-                            quantise_weight(
-                                wo_halves,
-                                C_IN // P,
-                                A_PASSES,
-                                wo_words[:].rearrange("p c r -> p (c r)"),
-                                wo_scales[:].rearrange("p c r -> p (c r)"),
-                            )
-                    if t == first_use - QUANT_LEAD:
-                        quantise_group(first_group + k, grouped[k])
-                if 0 <= t < len(side_loads):
-                    side_loads[t]()
-            side_loads = []
-        for t in range(LATE_TICKS):
-            tick(CHUNKS - 1, CHUNK_TILES + EXP_LEAD + t)
+        xj = [x_jobs(g) for g in range(N_GROUPS)]
+        wr = weight_jobs(wr_halves, A_DIM // P, 1, wr_words[:], wr_scales[:])
+        wo = weight_jobs(
+            wo_halves,
+            C_IN // P,
+            A_PASSES,
+            wo_words[:].rearrange("p c r -> p (c r)"),
+            wo_scales[:].rearrange("p c r -> p (c r)"),
+        )
+        jobs = JOBS(xj, wr, wo)
+
+        done = {"jobs": 0, "square": 0, "ratio": 0, "wkv": 0, "quant": 0, "project": 0, "store": 0}
+
+        def advance(what, upto, act):
+            while done[what] < upto:
+                act(done[what])
+                done[what] += 1
+
+        for n in range(N_TILES):
+            root(n)
+            if n + SUMK_AHEAD < N_TILES:
+                load_sumk(n + SUMK_AHEAD)
+            for load in side_loads.get(n, []):
+                load()
+            advance("wkv", min(A1 + W_LEAD, (n + 1 - SQ0 + W_EARLY) * A1 // (N_TILES - SQ0)), load_wkv)
+            advance("square", min(A1, done["wkv"], (n + 1 - SQ0) * A1 // (N_TILES - SQ0)), square)
+            advance("ratio", done["square"], ratio)
+            advance("jobs", min(len(jobs), (n + 1) * len(jobs) // PREP_T), lambda q: jobs[q]())
+            if n == R0_AT:
+                receptance(0)
+
+        for n in range(N_TILES + 20):
+            i = n - E_LAG
+            if n < N_TILES:
+                tanh(n)
+            if 0 <= i < N_TILES:
+                gate(i)
+            advance("store", done["project"], store)
+            ready = done["quant"]
+            if ready < len(QUANTS) and QUANT_END[ready] <= i - Q_LAG + 1:
+                advance("quant", ready + 1, quantise_gates)
+            advance("ratio", N_TILES if done["square"] == N_TILES else done["square"] - D_LAG, ratio)
+            if 0 <= i + 1 < N_TILES:
+                turn_ratio(i + 1)
+            if i >= N_TILES:
+                ready = done["quant"]
+            for m in range(1 if i < N_TILES - 2 else 2):
+                if done["project"] < N_TILES and QUANT_OF[done["project"]][0] < ready:
+                    advance("project", done["project"] + 1, project)
+            if n + 1 < N_TILES:
+                receptance(n + 1)
+            advance("wkv", min(N_TILES, done["ratio"] + W_AHEAD), load_wkv)
+            advance("square", min(N_TILES, A1 + (n + 1) * (N_TILES - A1) // SQ_T2), square)
+
+
+def JOBS(xj, wr, wo):
+    jobs = xj[0][:2] + wr[:1] + xj[0][2:5] + wr[1:4] + xj[1][:1] + xj[0][5:] + wr[4:]
+    jobs += xj[1][1:3] + wo[:2] + xj[1][3:5] + wo[2:4] + xj[2][:4] + xj[1][5:] + wo[4:] + xj[2][4:5]
+    jobs += xj[3][:1] + xj[2][5:]
+    for g in range(3, N_GROUPS):
+        jobs += xj[g][1:3] + (xj[g + 1][:1] if g + 1 < N_GROUPS else []) + xj[g][3:]
+    return jobs

@@ -167,9 +167,9 @@ def tile_rwkv2timemix_pa_t_kernel(tc, x, time_mix, Wr, wkv, sum_k, Wo, out):
                 nc.tensor.matmul(m_ps[:, j, :], lhsT=diags[:, 0, j, :], rhs=now[:, j, :], start=True, stop=False)
                 nc.tensor.matmul(m_ps[:, j, :], lhsT=diags[:, 1, j, :], rhs=before[:, j, :], start=False, stop=True)
             nc.vector.tensor_tensor(
-                out=grouped[g][:, P * n : P * (n + 1), :],
-                in0=m_ps[:].rearrange("p j t -> p t j"),
-                in1=before.rearrange("p j t -> p t j"),
+                out=grouped[g][:, P * n : P * (n + 1), :].rearrange("p (b i) j -> p b j i", i=4),
+                in0=m_ps[:].rearrange("p j (b i) -> p b j i", i=4),
+                in1=before.rearrange("p j (b i) -> p b j i", i=4),
                 op=ALU.add,
             )
 
@@ -279,7 +279,7 @@ def tile_rwkv2timemix_pa_t_kernel(tc, x, time_mix, Wr, wkv, sum_k, Wo, out):
         def root(i):
             ratio_tiles[i] = ratio_pool.tile([P, A_DIM], F32, name="ratio_t", tag="ratio")
             nc.scalar.activation(
-                out=ratio_tiles[i][:], in_=sumk_tiles[i][:], func=ACT.Abs_reciprocal_sqrt, scale=2.0
+                out=ratio_tiles[i][:], in_=sumk_tiles[i][:], func=ACT.Abs_reciprocal_sqrt
             )
 
         def square(i):
@@ -311,7 +311,7 @@ def tile_rwkv2timemix_pa_t_kernel(tc, x, time_mix, Wr, wkv, sum_k, Wo, out):
             tanh_tiles[i] = big_pool.tile([P, A_BLOCKS, P], F32, name="tanh_t", tag="big", align_bytes=64)
             for c in range(A_PASSES):
                 nc.scalar.activation(
-                    out=tanh_tiles[i][:, PACK * c : PACK * (c + 1), :], in_=r_banks[i, c][:], func=ACT.Tanh, scale=0.5
+                    out=tanh_tiles[i][:, PACK * c : PACK * (c + 1), :], in_=r_banks[i, c][:], func=ACT.Sigmoid
                 )
 
         def turn_ratio(i):
@@ -328,13 +328,11 @@ def tile_rwkv2timemix_pa_t_kernel(tc, x, time_mix, Wr, wkv, sum_k, Wo, out):
                     [P, QUANTS[k], A_PASSES, P, PACK], BF16, name="gate_t", tag="gate", align_bytes=64
                 )
             for c in range(A_PASSES):
-                nc.vector.scalar_tensor_tensor(
-                    out=gate_tiles[k][:, h, c, :, :],
-                    in0=tanh_tiles[i][:, PACK * c : PACK * (c + 1), :].rearrange("p j t -> p t j"),
-                    scalar=1.0,
-                    in1=ratio_banks[i, c][:].rearrange("p j t -> p t j"),
-                    op0=ALU.add,
-                    op1=ALU.mult,
+                nc.vector.tensor_tensor(
+                    out=gate_tiles[k][:, h, c, :, :].rearrange("p (b i) j -> p b j i", i=4),
+                    in0=tanh_tiles[i][:, PACK * c : PACK * (c + 1), :].rearrange("p j (b i) -> p b j i", i=4),
+                    in1=ratio_banks[i, c][:].rearrange("p j (b i) -> p b j i", i=4),
+                    op=ALU.mult,
                 )
 
         def quantise_gates(k):

@@ -34,6 +34,16 @@ PR = 4
 PO = 2
 SQ0 = 4
 A1 = 10
+REST = 5
+STAGE_G = 5
+WO_AT = 20
+WR_AT = 5
+X_AT = 2
+X_STEP = 4
+W_G = ()
+WR_POS = 2
+WO_POS = 7
+REST_RATE = 3
 W_LEAD = 2
 W_EARLY = 4
 PREP_T = 30
@@ -41,9 +51,13 @@ R0_AT = 25
 MGROUPS = (1, 3, 4, 5, 6, 7)
 E_LAG = 2
 SQ_T2 = 30
+SQ_DELAY = 0
+G_SQ = ()
 D_LAG = 1
 Q_LAG = 2
 S_LAST = 28
+SQ_LEAD = 2
+G_INTER = (0, 2)
 QUANTS = [4] * 7 + [2, 2]
 QUANT_OF = [(k, h) for k in range(len(QUANTS)) for h in range(QUANTS[k])]
 QUANT_END = [sum(QUANTS[: k + 1]) for k in range(len(QUANTS))]
@@ -59,7 +73,7 @@ def tile_rwkv2timemix_pa_t_kernel(tc, x, time_mix, Wr, wkv, sum_k, Wo, out):
     with ExitStack() as ctx:
         keep = ctx.enter_context(tc.tile_pool(name="keep", bufs=1))
         big_pool = ctx.enter_context(tc.tile_pool(name="big_pool", bufs=BIG))
-        xq_pool = ctx.enter_context(tc.tile_pool(name="xq_pool", bufs=N_GROUPS))
+        xq_pool = ctx.enter_context(tc.tile_pool(name="xq_pool", bufs=N_SEQ))
         in_pool = ctx.enter_context(tc.tile_pool(name="in_pool", bufs=IN_BUFS))
         ratio_pool = ctx.enter_context(tc.tile_pool(name="ratio_pool", bufs=N_TILES))
         gate_pool = ctx.enter_context(tc.tile_pool(name="gate_pool", bufs=2))
@@ -85,8 +99,13 @@ def tile_rwkv2timemix_pa_t_kernel(tc, x, time_mix, Wr, wkv, sum_k, Wo, out):
         def load_rows(dst, rows):
             nc.sync.dma_start(out=dst, in_=rows.rearrange("(n p) w -> p n w", p=P))
 
+        def stage(g, shape, dtype, name):
+            if g < STAGE_G:
+                return ratio_pool.tile(shape, dtype, name=name, tag="ratio", align_bytes=64)
+            return big_pool.tile(shape, dtype, name=name, tag="big", align_bytes=64)
+
         def load_x(g):
-            x_tiles[g] = big_pool.tile([P, GROUP_TILES, C_IN], BF16, name="x_t", tag="big", align_bytes=64)
+            x_tiles[g] = stage(g, [P, GROUP_TILES, C_IN], BF16, "x_t")
             for h in range(2):
                 r0 = GROUP * g + 2 * P * h
                 load_rows(x_tiles[g][:, 2 * h : 2 * h + 2, :], x_rows[r0 : r0 + 2 * P, :])
@@ -101,8 +120,7 @@ def tile_rwkv2timemix_pa_t_kernel(tc, x, time_mix, Wr, wkv, sum_k, Wo, out):
         mix_rows = keep.tile([P, P], BF16, name="mix_rows")
         nc.vector.memset(mix_rows[:], 0.0)
         nc.sync.dma_start(out=mix_rows[0:PACK, :], in_=time_mix.rearrange("a b (j p) -> (a b j) p", p=P))
-        for i in range(1, SUMK_AHEAD):
-            load_sumk(i)
+        load_sumk(1)
         mix_ps = psum_out.tile([P, P], BF16, name="mix_ps", tag="o_ps")
         nc.tensor.transpose(mix_ps[:], mix_rows[:], ident_bf[:])
         mix_col = keep.tile([P, PACK], F32, name="mix_col")
@@ -141,6 +159,12 @@ def tile_rwkv2timemix_pa_t_kernel(tc, x, time_mix, Wr, wkv, sum_k, Wo, out):
                     )
             return x_ps
 
+        def group_half(g):
+            s, h = divmod(g, 2)
+            if s not in grouped:
+                grouped[s] = gate_pool.tile([P, SEQ_LEN, PACK], BF16, name="grouped_t", tag="gate", align_bytes=64)
+            return grouped[s][:, GROUP * h : GROUP * (h + 1), :]
+
         def carry_last(g, pair, x_ps):
             if g % 2 == 0:
                 nc.vector.tensor_copy(
@@ -158,8 +182,6 @@ def tile_rwkv2timemix_pa_t_kernel(tc, x, time_mix, Wr, wkv, sum_k, Wo, out):
                 carry_last(g, pair, x_ps)
 
         def x_mix(g, n):
-            if n == 0:
-                grouped[g] = big_pool.tile([P, GROUP, PACK], BF16, name="grouped_t", tag="big", align_bytes=64)
             now = xts[g][:, :, PAD + P * n : PAD + P * (n + 1)]
             before = xts[g][:, :, PAD - 1 + P * n : PAD - 1 + P * (n + 1)]
             m_ps = psum_out.tile([P, PACK, P], F32, name="m_ps", tag="o_ps")
@@ -167,7 +189,7 @@ def tile_rwkv2timemix_pa_t_kernel(tc, x, time_mix, Wr, wkv, sum_k, Wo, out):
                 nc.tensor.matmul(m_ps[:, j, :], lhsT=diags[:, 0, j, :], rhs=now[:, j, :], start=True, stop=False)
                 nc.tensor.matmul(m_ps[:, j, :], lhsT=diags[:, 1, j, :], rhs=before[:, j, :], start=False, stop=True)
             nc.vector.tensor_tensor(
-                out=grouped[g][:, P * n : P * (n + 1), :].rearrange("p (b i) j -> p b j i", i=4),
+                out=group_half(g)[:, P * n : P * (n + 1), :].rearrange("p (b i) j -> p b j i", i=4),
                 in0=m_ps[:].rearrange("p j (b i) -> p b j i", i=4),
                 in1=before.rearrange("p j (b i) -> p b j i", i=4),
                 op=ALU.add,
@@ -179,14 +201,14 @@ def tile_rwkv2timemix_pa_t_kernel(tc, x, time_mix, Wr, wkv, sum_k, Wo, out):
             def carry(pair):
                 if pair == 0:
                     new_xt(g + 1)
-                    held["planes"] = big_pool.tile([P, PACK, GROUP], BF16, name="planes", tag="big", align_bytes=64)
-                    held["carry"] = gate_pool.tile([P, PACK, GROUP], F32, name="carry", tag="gate", align_bytes=64)
-                    nc.vector.memset(held["carry"][:, :, 0:1], 0.0)
+                    held["planes"] = stage(g, [P, PACK, GROUP], BF16, "planes")
+                held["carry"] = ratio_pool.tile([P, 2, GROUP], F32, name="carry_t", tag="ratio", align_bytes=64)
+                nc.vector.memset(held["carry"][:, :, 0:1], 0.0)
                 held[pair] = turn_x(g, pair)
                 for h in range(2):
                     j = 2 * pair + h
                     nc.vector.tensor_scalar_mul(
-                        out=held["carry"][:, j, 1:GROUP],
+                        out=held["carry"][:, h, 1:GROUP],
                         in0=held[pair][:, h, 0 : GROUP - 1],
                         scalar1=rest_col[:, j : j + 1],
                     )
@@ -199,90 +221,109 @@ def tile_rwkv2timemix_pa_t_kernel(tc, x, time_mix, Wr, wkv, sum_k, Wo, out):
                         out=held["planes"][:, j, :],
                         in0=held[pair][:, h, :],
                         scalar=mix_col[:, j : j + 1],
-                        in1=held["carry"][:, j, :],
+                        in1=held["carry"][:, h, :],
                         op0=ALU.mult,
                         op1=ALU.add,
                     )
 
             def interleave():
-                grouped[g] = big_pool.tile([P, GROUP, PACK], BF16, name="grouped_t", tag="big", align_bytes=64)
                 planes = held["planes"][:].rearrange("p j t -> p t j")
-                if g == 0:
+                if g in G_INTER:
                     nc.gpsimd.tensor_scalar(
-                        out=grouped[g][:], in0=planes, scalar1=1.0, scalar2=0.0, op0=ALU.mult, op1=ALU.add
+                        out=group_half(g), in0=planes, scalar1=1.0, scalar2=0.0, op0=ALU.mult, op1=ALU.add
                     )
                 else:
-                    nc.vector.tensor_copy(out=grouped[g][:], in_=planes)
+                    nc.vector.tensor_copy(out=group_half(g), in_=planes)
 
-            return [lambda: carry(0), lambda: mix(0), lambda: carry(1), lambda: mix(1), interleave, lambda: x_quant(g)]
+            return [lambda: carry(0), lambda: mix(0), lambda: carry(1), lambda: mix(1), interleave]
 
-        def x_quant(g):
-            x_words[g] = xq_pool.tile([P, GROUP], U32, name="x_words_t", align_bytes=64)
-            x_scales[g] = xq_pool.tile([P, GROUP], U8, name="x_scales_t", align_bytes=64)
+        def x_quant(s):
+            x_words[s] = xq_pool.tile([P, SEQ_LEN], U32, name="x_words_t", align_bytes=64)
+            x_scales[s] = xq_pool.tile([P, SEQ_LEN], U8, name="x_scales_t", align_bytes=64)
             nc.vector.quantize_mx(
-                out=x_words[g][:].bitcast(FP8X4),
-                scales=x_scales[g][:],
-                in_=grouped[g][:].rearrange("p t j -> p (t j)"),
+                out=x_words[s][:].bitcast(FP8X4),
+                scales=x_scales[s][:],
+                in_=grouped[s][:].rearrange("p t j -> p (t j)"),
             )
 
         def x_jobs(g):
             if g in MGROUPS:
-                return (
-                    [lambda: x_turn(g)] + [lambda n=n: x_mix(g, n) for n in range(GROUP_TILES)] + [lambda: x_quant(g)]
-                )
+                return [lambda: x_turn(g)] + [lambda n=n: x_mix(g, n) for n in range(GROUP_TILES)]
             return direct_jobs(g)
 
         def weight_loads(w, row_tiles, width):
             half_tiles = row_tiles // 2
             step = 2 * P * C_IN // width // P
-            halves = []
-            loads = []
-            for h in range(2):
-                w_t = ratio_pool.tile([P, half_tiles, width], BF16, name="w_t", tag="ratio")
-                halves.append(w_t)
-                for s in range(0, half_tiles, step):
-                    r0 = P * (half_tiles * h + s)
-                    loads.append(
-                        lambda dst=w_t[:, s : s + step, :], rows=w[r0 : r0 + P * step, :]: load_rows(dst, rows)
-                    )
-            return halves, loads
+            halves = {}
 
-        def weight_jobs(halves, row_tiles, passes, words, scales):
+            def load(h, s):
+                if s == 0:
+                    pool, tag = (ratio_pool, "ratio") if width == C_IN else (big_pool, "big")
+                    halves[h] = pool.tile([P, half_tiles, width], BF16, name="w_t", tag=tag, align_bytes=64)
+                r0 = P * (half_tiles * h + s)
+                load_rows(halves[h][:, s : s + step, :], w[r0 : r0 + P * step, :])
+
+            return halves, [lambda h=h, s=s: load(h, s) for h in range(2) for s in range(0, half_tiles, step)]
+
+        def weight_jobs(name, halves, row_tiles, passes, words, scales):
             units = [(c, m) for c in range(passes) for m in range(row_tiles)]
-            held = []
+            held = {}
 
             def turn(pair):
                 if pair == 0:
-                    held.append(
-                        gate_pool.tile([P, len(units) * P, PACK], BF16, name="grouped_w", tag="gate", align_bytes=64)
+                    held["grouped"] = gate_pool.tile(
+                        [P, len(units) * P, PACK], BF16, name="grouped_w", tag="gate", align_bytes=64
                     )
-                grouped_w = held[0]
-                w_ps = psum_turn.tile([P, 2, PACK, P], BF16, name="w_ps", tag="turn")
+                if name in W_G and pair % 2 == 0:
+                    held["planes"] = ratio_pool.tile([P, PACK, 4 * P], BF16, name="planes_w", tag="ratio", align_bytes=64)
+                w_ps = psum_turn.tile([P, PACK, 2, P], BF16, name="w_ps", tag="turn")
                 for h in range(2):
                     c, m = units[2 * pair + h]
                     w_t = halves[m // (row_tiles // 2)]
                     for j in range(PACK):
                         k0 = K_PASS * c + P * j
-                        nc.tensor.transpose(w_ps[:, h, j, :], w_t[:, m % (row_tiles // 2), k0 : k0 + P], ident_bf[:])
+                        nc.tensor.transpose(w_ps[:, j, h, :], w_t[:, m % (row_tiles // 2), k0 : k0 + P], ident_bf[:])
+                if name not in W_G:
+                    nc.vector.tensor_copy(
+                        out=held["grouped"][:, 2 * P * pair : 2 * P * (pair + 1), :].rearrange(
+                            "p (b i) j -> p b j i", i=4
+                        ),
+                        in_=w_ps[:].rearrange("p j h (b i) -> p (h b) j i", i=4),
+                    )
+                    return
                 nc.vector.tensor_copy(
-                    out=grouped_w[:, 2 * P * pair : 2 * P * (pair + 1), :].rearrange("p (h r) j -> p h r j", h=2),
-                    in_=w_ps[:].rearrange("p h j r -> p h r j"),
+                    out=held["planes"][:, :, 2 * P * (pair % 2) : 2 * P * (pair % 2 + 1)],
+                    in_=w_ps[:].rearrange("p j h r -> p j (h r)"),
                 )
+                if pair % 2 == 1:
+                    nc.gpsimd.tensor_scalar(
+                        out=held["grouped"][:, 4 * P * (pair // 2) : 4 * P * (pair // 2 + 1), :],
+                        in0=held["planes"][:].rearrange("p j r -> p r j"),
+                        scalar1=1.0,
+                        scalar2=0.0,
+                        op0=ALU.mult,
+                        op1=ALU.add,
+                    )
 
             def quant():
                 nc.vector.quantize_mx(
-                    out=words.bitcast(FP8X4), scales=scales, in_=held[0][:].rearrange("p r j -> p (r j)")
+                    out=words.bitcast(FP8X4), scales=scales, in_=held["grouped"][:].rearrange("p r j -> p (r j)")
                 )
 
             return [lambda q=q: turn(q) for q in range(len(units) // 2)] + [quant]
 
         def root(i):
-            ratio_tiles[i] = ratio_pool.tile([P, A_DIM], F32, name="ratio_t", tag="ratio")
+            ratio_tiles[i] = ratio_pool.tile([P, A_DIM], F32, name="ratio_t", tag="ratio", align_bytes=64)
             nc.scalar.activation(
                 out=ratio_tiles[i][:], in_=sumk_tiles[i][:], func=ACT.Abs_reciprocal_sqrt
             )
 
         def square(i):
+            if i in G_SQ:
+                nc.gpsimd.tensor_tensor(
+                    out=ratio_tiles[i][:], in0=ratio_tiles[i][:], in1=ratio_tiles[i][:], op=ALU.mult
+                )
+                return
             nc.scalar.activation(out=ratio_tiles[i][:], in_=ratio_tiles[i][:], func=ACT.Square)
 
         def ratio(i):
@@ -290,48 +331,53 @@ def tile_rwkv2timemix_pa_t_kernel(tc, x, time_mix, Wr, wkv, sum_k, Wo, out):
                 out=ratio_tiles[i][:], in0=wkv_tiles[i][:], in1=ratio_tiles[i][:], op=ALU.mult
             )
 
-        def receptance(i):
-            g = i // GROUP_TILES
-            t0 = P * (i % GROUP_TILES)
-            for c in range(A_PASSES):
-                r_banks[i, c] = psum_r.tile([P, PACK, P], F32, name="r_ps")
-                for j in range(PACK):
-                    a0 = K_PASS * c + P * j
+        def receptance(u):
+            k, c = divmod(u, A_PASSES)
+            g, part = divmod(k, N_TILES // N_SEQ // 2)
+            t0 = 2 * P * part
+            for b in range(2):
+                r_banks[u, b] = psum_r.tile([P, 2, 2 * P], F32, name="r_ps")
+                for h in range(2):
+                    a0 = K_PASS * c + P * (2 * b + h)
                     nc.tensor.matmul_mx(
-                        out=r_banks[i, c][:, j, :],
+                        out=r_banks[u, b][:, h, :],
                         lhsT=wr_words[:, a0 : a0 + P].bitcast(FP8X4),
                         lhsT_scale=wr_scales[:, a0 : a0 + P],
-                        rhs=x_words[g][:, t0 : t0 + P].bitcast(FP8X4),
-                        rhs_scale=x_scales[g][:, t0 : t0 + P],
+                        rhs=x_words[g][:, t0 : t0 + 2 * P].bitcast(FP8X4),
+                        rhs_scale=x_scales[g][:, t0 : t0 + 2 * P],
                         start=True,
                         stop=True,
                     )
 
-        def tanh(i):
-            tanh_tiles[i] = big_pool.tile([P, A_BLOCKS, P], F32, name="tanh_t", tag="big", align_bytes=64)
-            for c in range(A_PASSES):
+        def tanh(u):
+            tanh_tiles[u] = big_pool.tile([P, PACK, 2 * P], F32, name="tanh_t", tag="big", align_bytes=64)
+            for b in range(2):
                 nc.scalar.activation(
-                    out=tanh_tiles[i][:, PACK * c : PACK * (c + 1), :], in_=r_banks[i, c][:], func=ACT.Sigmoid
+                    out=tanh_tiles[u][:, 2 * b : 2 * b + 2, :], in_=r_banks[u, b][:], func=ACT.Sigmoid
                 )
 
-        def turn_ratio(i):
-            for c in range(A_PASSES):
-                ratio_banks[i, c] = psum_turn.tile([P, PACK, P], F32, name="ratio_ps", tag="turn")
+        def turn_ratio(u):
+            k, c = divmod(u, A_PASSES)
+            for h in range(2):
+                ratio_banks[u, h] = psum_turn.tile([P, PACK, P], F32, name="ratio_ps", tag="turn")
                 for j in range(PACK):
                     a0 = K_PASS * c + P * j
-                    nc.tensor.transpose(ratio_banks[i, c][:, j, :], ratio_tiles[i][:, a0 : a0 + P], ident_f32[:])
+                    nc.tensor.transpose(
+                        ratio_banks[u, h][:, j, :], ratio_tiles[2 * k + h][:, a0 : a0 + P], ident_f32[:]
+                    )
 
-        def gate(i):
-            k, h = QUANT_OF[i]
-            if h == 0:
-                gate_tiles[k] = gate_pool.tile(
-                    [P, QUANTS[k], A_PASSES, P, PACK], BF16, name="gate_t", tag="gate", align_bytes=64
-                )
-            for c in range(A_PASSES):
+        def gate(u):
+            k, c = divmod(u, A_PASSES)
+            for h in range(2):
+                q, m = QUANT_OF[2 * k + h]
+                if c == 0 and m == 0:
+                    gate_tiles[q] = gate_pool.tile(
+                        [P, QUANTS[q], A_PASSES, P, PACK], BF16, name="gate_t", tag="gate", align_bytes=64
+                    )
                 nc.vector.tensor_tensor(
-                    out=gate_tiles[k][:, h, c, :, :].rearrange("p (b i) j -> p b j i", i=4),
-                    in0=tanh_tiles[i][:, PACK * c : PACK * (c + 1), :].rearrange("p j (b i) -> p b j i", i=4),
-                    in1=ratio_banks[i, c][:].rearrange("p j (b i) -> p b j i", i=4),
+                    out=gate_tiles[q][:, m, c, :, :].rearrange("p (b i) j -> p b j i", i=4),
+                    in0=tanh_tiles[u][:, :, P * h : P * (h + 1)].rearrange("p j (b i) -> p b j i", i=4),
+                    in1=ratio_banks[u, h][:].rearrange("p j (b i) -> p b j i", i=4),
                     op=ALU.mult,
                 )
 
@@ -368,21 +414,27 @@ def tile_rwkv2timemix_pa_t_kernel(tc, x, time_mix, Wr, wkv, sum_k, Wo, out):
 
         wr_halves, wr_loads = weight_loads(Wr, A_DIM // P, C_IN)
         wo_halves, wo_loads = weight_loads(Wo, C_IN // P, A_DIM)
-        side_loads = {0: wr_loads[0:1], 1: wr_loads[1:2], 2: wr_loads[2:3], 3: wr_loads[3:4], 6: wo_loads[0:2], 8: wo_loads[2:4]}
-        side_loads[4] = [lambda: load_x(1)]
+        load_sumk(2)
+        load_x(1)
+        for i in range(3, SUMK_AHEAD + 1):
+            load_sumk(i)
+        side_loads = {WO_AT + q: wo_loads[q : q + 1] for q in range(4)}
+        for q in range(4):
+            side_loads.setdefault(WR_AT + q, []).append(wr_loads[q])
         for g in range(2, N_GROUPS):
-            side_loads[4 + 3 * g] = [lambda g=g: load_x(g)]
+            side_loads.setdefault(X_AT + X_STEP * (g - 2), []).append(lambda g=g: load_x(g))
 
         xj = [x_jobs(g) for g in range(N_GROUPS)]
-        wr = weight_jobs(wr_halves, A_DIM // P, 1, wr_words[:], wr_scales[:])
+        wr = weight_jobs("wr", wr_halves, A_DIM // P, 1, wr_words[:], wr_scales[:])
         wo = weight_jobs(
+            "wo",
             wo_halves,
             C_IN // P,
             A_PASSES,
             wo_words[:].rearrange("p c r -> p (c r)"),
             wo_scales[:].rearrange("p c r -> p (c r)"),
         )
-        jobs = JOBS(xj, wr, wo)
+        jobs = JOBS(xj, wr, wo, [lambda s=s: x_quant(s) for s in range(N_SEQ)])
 
         done = {"jobs": 0, "square": 0, "ratio": 0, "wkv": 0, "quant": 0, "project": 0, "store": 0}
 
@@ -393,14 +445,14 @@ def tile_rwkv2timemix_pa_t_kernel(tc, x, time_mix, Wr, wkv, sum_k, Wo, out):
 
         for n in range(N_TILES):
             root(n)
-            if n + SUMK_AHEAD < N_TILES:
+            if n > 0 and n + SUMK_AHEAD < N_TILES:
                 load_sumk(n + SUMK_AHEAD)
             for load in side_loads.get(n, []):
                 load()
             advance("wkv", min(A1 + W_LEAD, (n + 1 - SQ0 + W_EARLY) * A1 // (N_TILES - SQ0)), load_wkv)
             advance("square", min(A1, done["wkv"], (n + 1 - SQ0) * A1 // (N_TILES - SQ0)), square)
             advance("ratio", done["square"], ratio)
-            advance("jobs", min(len(jobs), (n + 1) * len(jobs) // PREP_T), lambda q: jobs[q]())
+            advance("jobs", min(len(jobs) - REST, (n + 1) * (len(jobs) - REST) // PREP_T), lambda q: jobs[q]())
             if n == R0_AT:
                 receptance(0)
 
@@ -408,6 +460,7 @@ def tile_rwkv2timemix_pa_t_kernel(tc, x, time_mix, Wr, wkv, sum_k, Wo, out):
             i = n - E_LAG
             if n < N_TILES:
                 tanh(n)
+            advance("jobs", min(len(jobs), len(jobs) - REST + (n + 1) * REST_RATE), lambda q: jobs[q]())
             if 0 <= i < N_TILES:
                 gate(i)
             advance("store", done["project"], store)
@@ -425,13 +478,19 @@ def tile_rwkv2timemix_pa_t_kernel(tc, x, time_mix, Wr, wkv, sum_k, Wo, out):
             if n + 1 < N_TILES:
                 receptance(n + 1)
             advance("wkv", min(N_TILES, done["ratio"] + W_AHEAD), load_wkv)
-            advance("square", min(N_TILES, A1 + (n + 1) * (N_TILES - A1) // SQ_T2), square)
+            advance("square", min(N_TILES, A1 + max(0, n + 1 - SQ_DELAY) * (N_TILES - A1) // (SQ_T2 - SQ_DELAY)), square)
 
 
-def JOBS(xj, wr, wo):
-    jobs = xj[0][:2] + wr[:1] + xj[0][2:5] + wr[1:4] + xj[1][:1] + xj[0][5:] + wr[4:]
-    jobs += xj[1][1:3] + wo[:2] + xj[1][3:5] + wo[2:4] + xj[2][:4] + xj[1][5:] + wo[4:] + xj[2][4:5]
-    jobs += xj[3][:1] + xj[2][5:]
-    for g in range(3, N_GROUPS):
-        jobs += xj[g][1:3] + (xj[g + 1][:1] if g + 1 < N_GROUPS else []) + xj[g][3:]
+def JOBS(xj, wr, wo, quants):
+    jobs = []
+    waiting = []
+    for g in range(N_GROUPS):
+        body = xj[g][1:] if g > 0 else xj[g]
+        nxt = xj[g + 1][:1] if g + 1 < N_GROUPS else []
+        jobs += body[:2] + waiting + body[2:3] + nxt + body[3:]
+        waiting = quants[g // 2 : g // 2 + 1] if g % 2 == 1 else []
+        if g == WR_POS:
+            jobs += wr[:4]
+            waiting = waiting + wr[4:]
+    jobs += waiting + wo
     return jobs

@@ -26,9 +26,9 @@ N_GROUPS = N_TILES // GROUP_TILES
 PAD = 2
 SUMK_AHEAD = 5
 W_AHEAD = 6
-IN_BUFS = 7
-BIG = 7
-OB = 4
+IN_BUFS = 6
+WB = 6
+BIG = 8
 PA = 2
 PR = 4
 PO = 2
@@ -75,10 +75,10 @@ def tile_rwkv2timemix_pa_t_kernel(tc, x, time_mix, Wr, wkv, sum_k, Wo, out):
         big_pool = ctx.enter_context(tc.tile_pool(name="big_pool", bufs=BIG))
         xq_pool = ctx.enter_context(tc.tile_pool(name="xq_pool", bufs=N_SEQ))
         in_pool = ctx.enter_context(tc.tile_pool(name="in_pool", bufs=IN_BUFS))
+        w_pool = ctx.enter_context(tc.tile_pool(name="w_pool", bufs=WB))
         ratio_pool = ctx.enter_context(tc.tile_pool(name="ratio_pool", bufs=N_TILES))
         gate_pool = ctx.enter_context(tc.tile_pool(name="gate_pool", bufs=2))
         gq_pool = ctx.enter_context(tc.tile_pool(name="gq_pool", bufs=2))
-        o_pool = ctx.enter_context(tc.tile_pool(name="o_pool", bufs=OB))
         psum_r = ctx.enter_context(tc.psum_pool(name="psum_r", bufs=PA))
         psum_turn = ctx.enter_context(tc.psum_pool(name="psum_turn", bufs=PR))
         psum_out = ctx.enter_context(tc.psum_pool(name="psum_out", bufs=PO))
@@ -93,7 +93,7 @@ def tile_rwkv2timemix_pa_t_kernel(tc, x, time_mix, Wr, wkv, sum_k, Wo, out):
             nc.sync.dma_start(out=sumk_tiles[i][:], in_=sumk_rows[P * i : P * (i + 1), :])
 
         def load_wkv(i):
-            wkv_tiles[i] = in_pool.tile([P, A_DIM], BF16, name="wkv_t", tag="in")
+            wkv_tiles[i] = w_pool.tile([P, A_DIM], BF16, name="wkv_t")
             nc.sync.dma_start(out=wkv_tiles[i][:], in_=wkv_rows[P * i : P * (i + 1), :])
 
         def load_rows(dst, rows):
@@ -382,7 +382,9 @@ def tile_rwkv2timemix_pa_t_kernel(tc, x, time_mix, Wr, wkv, sum_k, Wo, out):
                 )
 
         def quantise_gates(k):
-            gate_words[k] = gq_pool.tile([P, QUANTS[k], A_PASSES, P], U32, name="gate_words_t", align_bytes=64)
+            gate_words[k] = big_pool.tile(
+                [P, QUANTS[k], A_PASSES, P], U32, name="gate_words_t", tag="big", align_bytes=64
+            )
             gate_scales[k] = gq_pool.tile([P, QUANTS[k], A_PASSES, P], U8, name="gate_scales_t", align_bytes=64)
             nc.vector.quantize_mx(
                 out=gate_words[k][:].rearrange("p q c t -> p (q c t)").bitcast(FP8X4),
@@ -405,7 +407,7 @@ def tile_rwkv2timemix_pa_t_kernel(tc, x, time_mix, Wr, wkv, sum_k, Wo, out):
                 )
 
         def store(i):
-            o_sb = o_pool.tile([P, C_IN], F32, name="o_sb")
+            o_sb = in_pool.tile([P, C_IN], F32, name="o_sb", tag="in")
             if i >= S_LAST:
                 nc.scalar.copy(out=o_sb[:], in_=out_banks[i][:])
             else:

@@ -24,16 +24,15 @@ GROUP = 512
 GROUP_TILES = GROUP // P
 N_GROUPS = N_TILES // GROUP_TILES
 PAD = 2
-SUMK_AHEAD = 5
 W_AHEAD = 6
-IN_BUFS = 6
-WB = 6
-BIG = 8
+IN_BUFS = 4
+WB = 3
+BIG = 7
 PA = 2
 PR = 4
 PO = 2
 SQ0 = 4
-A1 = 10
+A1 = 9
 REST = 5
 STAGE_G = 5
 WO_AT = 20
@@ -50,12 +49,13 @@ PREP_T = 30
 R0_AT = 25
 MGROUPS = (1, 3, 4, 5, 6, 7)
 E_LAG = 2
-SQ_T2 = 30
-SQ_DELAY = 0
+SQ_TICKS = (0, 1, 3)
+SQ_MORE = 0
 G_SQ = ()
 D_LAG = 1
 Q_LAG = 2
-S_LAST = 28
+S_LAST = 24
+PE_ORDER = "TPR"
 SQ_LEAD = 2
 G_INTER = (0, 2)
 QUANTS = [4] * 7 + [2, 2]
@@ -86,15 +86,20 @@ def tile_rwkv2timemix_pa_t_kernel(tc, x, time_mix, Wr, wkv, sum_k, Wo, out):
 
         sumk_tiles, wkv_tiles, ratio_tiles, x_tiles, xts, grouped = {}, {}, {}, {}, {}, {}
         x_words, x_scales, tanh_tiles, r_banks, ratio_banks = {}, {}, {}, {}, {}
-        gate_tiles, gate_words, gate_scales, out_banks = {}, {}, {}, {}
+        gate_tiles, gate_words, gate_scales, out_banks, out_tiles = {}, {}, {}, {}, {}
 
-        def load_sumk(i):
-            sumk_tiles[i] = in_pool.tile([P, A_DIM], BF16, name="sumk_t", tag="in")
-            nc.sync.dma_start(out=sumk_tiles[i][:], in_=sumk_rows[P * i : P * (i + 1), :])
+        def pair_rows(rows, k):
+            g, h = divmod(k, 2)
+            group = rows[GROUP * g : GROUP * (g + 1), :].rearrange("(p n) w -> p n w", n=GROUP_TILES)
+            return group[:, 2 * h : 2 * h + 2, :]
 
-        def load_wkv(i):
-            wkv_tiles[i] = w_pool.tile([P, A_DIM], BF16, name="wkv_t")
-            nc.sync.dma_start(out=wkv_tiles[i][:], in_=wkv_rows[P * i : P * (i + 1), :])
+        def load_sumk(k):
+            sumk_tiles[k] = in_pool.tile([P, 2, A_DIM], BF16, name="sumk_t", tag="in")
+            nc.sync.dma_start(out=sumk_tiles[k][:], in_=pair_rows(sumk_rows, k))
+
+        def load_wkv(k):
+            wkv_tiles[k] = w_pool.tile([P, 2, A_DIM], BF16, name="wkv_t")
+            nc.sync.dma_start(out=wkv_tiles[k][:], in_=pair_rows(wkv_rows, k))
 
         def load_rows(dst, rows):
             nc.sync.dma_start(out=dst, in_=rows.rearrange("(n p) w -> p n w", p=P))
@@ -106,21 +111,22 @@ def tile_rwkv2timemix_pa_t_kernel(tc, x, time_mix, Wr, wkv, sum_k, Wo, out):
 
         def load_x(g):
             x_tiles[g] = stage(g, [P, GROUP_TILES, C_IN], BF16, "x_t")
-            for h in range(2):
-                r0 = GROUP * g + 2 * P * h
-                load_rows(x_tiles[g][:, 2 * h : 2 * h + 2, :], x_rows[r0 : r0 + 2 * P, :])
+            rows = x_rows[GROUP * g : GROUP * (g + 1), :].rearrange("(p n) w -> p n w", n=GROUP_TILES)
+            nc.sync.dma_start(out=x_tiles[g][:], in_=rows)
 
         ident_bf = keep.tile([P, P], BF16, name="ident_bf")
         make_identity(nc, ident_bf[:])
         ident_f32 = keep.tile([P, P], F32, name="ident_f32")
         make_identity(nc, ident_f32[:])
 
-        load_sumk(0)
-        load_x(0)
+        sumk_tiles[0] = in_pool.tile([P, 2, A_DIM], BF16, name="sumk_t", tag="in")
+        first_sumk = pair_rows(sumk_rows, 0)
+        nc.sync.dma_start(out=sumk_tiles[0][:, 0, :], in_=first_sumk[:, 0, :])
         mix_rows = keep.tile([P, P], BF16, name="mix_rows")
         nc.vector.memset(mix_rows[:], 0.0)
         nc.sync.dma_start(out=mix_rows[0:PACK, :], in_=time_mix.rearrange("a b (j p) -> (a b j) p", p=P))
-        load_sumk(1)
+        load_x(0)
+        nc.sync.dma_start(out=sumk_tiles[0][:, 1, :], in_=first_sumk[:, 1, :])
         mix_ps = psum_out.tile([P, P], BF16, name="mix_ps", tag="o_ps")
         nc.tensor.transpose(mix_ps[:], mix_rows[:], ident_bf[:])
         mix_col = keep.tile([P, PACK], F32, name="mix_col")
@@ -149,13 +155,14 @@ def tile_rwkv2timemix_pa_t_kernel(tc, x, time_mix, Wr, wkv, sum_k, Wo, out):
         def new_xt(g):
             xts[g] = big_pool.tile([P, PACK, GROUP + PAD], BF16, name="xt", tag="big", align_bytes=64)
 
-        def turn_x(g, pair):
+        def turn_x(g, pair, first):
             x_ps = psum_turn.tile([P, 2, GROUP], BF16, name="x_ps", tag="turn")
             for h in range(2):
                 j = 2 * pair + h
-                for n in range(GROUP_TILES):
+                for m in range(GROUP_TILES):
+                    n = (first + m) % GROUP_TILES
                     nc.tensor.transpose(
-                        x_ps[:, h, P * n : P * (n + 1)], x_tiles[g][:, n, P * j : P * (j + 1)], ident_bf[:]
+                        x_ps[:, h, P * m : P * (m + 1)], x_tiles[g][:, n, P * j : P * (j + 1)], ident_bf[:]
                     )
             return x_ps
 
@@ -165,10 +172,10 @@ def tile_rwkv2timemix_pa_t_kernel(tc, x, time_mix, Wr, wkv, sum_k, Wo, out):
                 grouped[s] = gate_pool.tile([P, SEQ_LEN, PACK], BF16, name="grouped_t", tag="gate", align_bytes=64)
             return grouped[s][:, GROUP * h : GROUP * (h + 1), :]
 
-        def carry_last(g, pair, x_ps):
+        def carry_last(g, pair, x_ps, end):
             if g % 2 == 0:
                 nc.vector.tensor_copy(
-                    out=xts[g + 1][:, 2 * pair : 2 * pair + 2, 0:PAD], in_=x_ps[:, :, GROUP - PAD : GROUP]
+                    out=xts[g + 1][:, 2 * pair : 2 * pair + 2, 0:PAD], in_=x_ps[:, :, end - PAD : end]
                 )
 
         def x_turn(g):
@@ -177,13 +184,15 @@ def tile_rwkv2timemix_pa_t_kernel(tc, x, time_mix, Wr, wkv, sum_k, Wo, out):
                 nc.vector.memset(xts[g][:, :, 0:PAD], 0.0)
                 new_xt(g + 1)
             for pair in range(2):
-                x_ps = turn_x(g, pair)
+                x_ps = turn_x(g, pair, GROUP_TILES - 1)
                 nc.vector.tensor_copy(out=xts[g][:, 2 * pair : 2 * pair + 2, PAD : PAD + GROUP], in_=x_ps[:])
-                carry_last(g, pair, x_ps)
+                carry_last(g, pair, x_ps, P)
 
         def x_mix(g, n):
-            now = xts[g][:, :, PAD + P * n : PAD + P * (n + 1)]
-            before = xts[g][:, :, PAD - 1 + P * n : PAD - 1 + P * (n + 1)]
+            a = PAD + P * ((n + 1) % GROUP_TILES)
+            b = PAD + P * n - (1 if n == 0 else 0)
+            now = xts[g][:, :, a : a + P]
+            before = xts[g][:, :, b : b + P]
             m_ps = psum_out.tile([P, PACK, P], F32, name="m_ps", tag="o_ps")
             for j in range(PACK):
                 nc.tensor.matmul(m_ps[:, j, :], lhsT=diags[:, 0, j, :], rhs=now[:, j, :], start=True, stop=False)
@@ -204,15 +213,14 @@ def tile_rwkv2timemix_pa_t_kernel(tc, x, time_mix, Wr, wkv, sum_k, Wo, out):
                     held["planes"] = stage(g, [P, PACK, GROUP], BF16, "planes")
                 held["carry"] = ratio_pool.tile([P, 2, GROUP], F32, name="carry_t", tag="ratio", align_bytes=64)
                 nc.vector.memset(held["carry"][:, :, 0:1], 0.0)
-                held[pair] = turn_x(g, pair)
+                held[pair] = turn_x(g, pair, 0)
                 for h in range(2):
                     j = 2 * pair + h
-                    nc.vector.tensor_scalar_mul(
-                        out=held["carry"][:, h, 1:GROUP],
-                        in0=held[pair][:, h, 0 : GROUP - 1],
-                        scalar1=rest_col[:, j : j + 1],
-                    )
-                carry_last(g, pair, held[pair])
+                    for dst, src in ((slice(1, P), slice(GROUP - P, GROUP - 1)), (slice(P, GROUP), slice(0, GROUP - P))):
+                        nc.vector.tensor_scalar_mul(
+                            out=held["carry"][:, h, dst], in0=held[pair][:, h, src], scalar1=rest_col[:, j : j + 1]
+                        )
+                carry_last(g, pair, held[pair], GROUP)
 
             def mix(pair):
                 for h in range(2):
@@ -315,7 +323,7 @@ def tile_rwkv2timemix_pa_t_kernel(tc, x, time_mix, Wr, wkv, sum_k, Wo, out):
         def root(i):
             ratio_tiles[i] = ratio_pool.tile([P, A_DIM], F32, name="ratio_t", tag="ratio", align_bytes=64)
             nc.scalar.activation(
-                out=ratio_tiles[i][:], in_=sumk_tiles[i][:], func=ACT.Abs_reciprocal_sqrt
+                out=ratio_tiles[i][:], in_=sumk_tiles[i // 2][:, i % 2, :], func=ACT.Abs_reciprocal_sqrt
             )
 
         def square(i):
@@ -328,7 +336,7 @@ def tile_rwkv2timemix_pa_t_kernel(tc, x, time_mix, Wr, wkv, sum_k, Wo, out):
 
         def ratio(i):
             nc.gpsimd.tensor_tensor(
-                out=ratio_tiles[i][:], in0=wkv_tiles[i][:], in1=ratio_tiles[i][:], op=ALU.mult
+                out=ratio_tiles[i][:], in0=wkv_tiles[i // 2][:, i % 2, :], in1=ratio_tiles[i][:], op=ALU.mult
             )
 
         def receptance(u):
@@ -407,19 +415,24 @@ def tile_rwkv2timemix_pa_t_kernel(tc, x, time_mix, Wr, wkv, sum_k, Wo, out):
                 )
 
         def store(i):
-            o_sb = in_pool.tile([P, C_IN], F32, name="o_sb", tag="in")
+            k, h = divmod(i, 2)
+            if h == 0:
+                out_tiles[k] = in_pool.tile([P, 2, C_IN], F32, name="o_sb", tag="in")
             if i >= S_LAST:
-                nc.scalar.copy(out=o_sb[:], in_=out_banks[i][:])
+                nc.scalar.copy(out=out_tiles[k][:, h, :], in_=out_banks[i][:])
             else:
-                nc.vector.tensor_copy(out=o_sb[:], in_=out_banks[i][:])
-            nc.sync.dma_start(out=out_rows[P * i : P * (i + 1), :], in_=o_sb[:])
+                nc.vector.tensor_copy(out=out_tiles[k][:, h, :], in_=out_banks[i][:])
+            dst = pair_rows(out_rows, k)
+            if k == N_TILES // 2 - 1:
+                nc.sync.dma_start(out=dst[:, h, :], in_=out_tiles[k][:, h, :])
+            elif h == 1:
+                nc.sync.dma_start(out=dst, in_=out_tiles[k][:])
 
         wr_halves, wr_loads = weight_loads(Wr, A_DIM // P, C_IN)
         wo_halves, wo_loads = weight_loads(Wo, C_IN // P, A_DIM)
-        load_sumk(2)
+        load_sumk(1)
         load_x(1)
-        for i in range(3, SUMK_AHEAD + 1):
-            load_sumk(i)
+        load_sumk(2)
         side_loads = {WO_AT + q: wo_loads[q : q + 1] for q in range(4)}
         for q in range(4):
             side_loads.setdefault(WR_AT + q, []).append(wr_loads[q])
@@ -447,12 +460,12 @@ def tile_rwkv2timemix_pa_t_kernel(tc, x, time_mix, Wr, wkv, sum_k, Wo, out):
 
         for n in range(N_TILES):
             root(n)
-            if n > 0 and n + SUMK_AHEAD < N_TILES:
-                load_sumk(n + SUMK_AHEAD)
+            if n % 2 == 1 and n // 2 + 3 < N_TILES // 2:
+                load_sumk(n // 2 + 3)
             for load in side_loads.get(n, []):
                 load()
-            advance("wkv", min(A1 + W_LEAD, (n + 1 - SQ0 + W_EARLY) * A1 // (N_TILES - SQ0)), load_wkv)
-            advance("square", min(A1, done["wkv"], (n + 1 - SQ0) * A1 // (N_TILES - SQ0)), square)
+            advance("wkv", min(A1 + W_LEAD, (n + 1 - SQ0 + W_EARLY) * A1 // (N_TILES - SQ0) + 1) // 2, load_wkv)
+            advance("square", min(A1, 2 * done["wkv"], (n + 1 - SQ0) * A1 // (N_TILES - SQ0)), square)
             advance("ratio", done["square"], ratio)
             advance("jobs", min(len(jobs) - REST, (n + 1) * (len(jobs) - REST) // PREP_T), lambda q: jobs[q]())
             if n == R0_AT:
@@ -470,17 +483,19 @@ def tile_rwkv2timemix_pa_t_kernel(tc, x, time_mix, Wr, wkv, sum_k, Wo, out):
             if ready < len(QUANTS) and QUANT_END[ready] <= i - Q_LAG + 1:
                 advance("quant", ready + 1, quantise_gates)
             advance("ratio", N_TILES if done["square"] == N_TILES else done["square"] - D_LAG, ratio)
-            if 0 <= i + 1 < N_TILES:
-                turn_ratio(i + 1)
             if i >= N_TILES:
                 ready = done["quant"]
-            for m in range(1 if i < N_TILES - 2 else 2):
-                if done["project"] < N_TILES and QUANT_OF[done["project"]][0] < ready:
-                    advance("project", done["project"] + 1, project)
-            if n + 1 < N_TILES:
-                receptance(n + 1)
-            advance("wkv", min(N_TILES, done["ratio"] + W_AHEAD), load_wkv)
-            advance("square", min(N_TILES, A1 + max(0, n + 1 - SQ_DELAY) * (N_TILES - A1) // (SQ_T2 - SQ_DELAY)), square)
+            for what in PE_ORDER:
+                if what == "T" and 0 <= i + 1 < N_TILES:
+                    turn_ratio(i + 1)
+                if what == "P":
+                    for m in range(1 if i < N_TILES - 2 else 2):
+                        if done["project"] < N_TILES and QUANT_OF[done["project"]][0] < ready:
+                            advance("project", done["project"] + 1, project)
+                if what == "R" and n + 1 < N_TILES:
+                    receptance(n + 1)
+            advance("wkv", min(N_TILES, done["ratio"] + W_AHEAD) // 2, load_wkv)
+            advance("square", min(N_TILES, A1 + SQ_MORE + sum(1 for m in range(n + 1) if m % 4 in SQ_TICKS)), square)
 
 
 def JOBS(xj, wr, wo, quants):

@@ -54,7 +54,10 @@ SQ_MORE = 0
 G_SQ = ()
 D_LAG = 1
 Q_LAG = 2
-S_LAST = 24
+S_COPIES = range(22, 31)
+P2_AT = 28
+LAST_Q = 1
+LAST_LAG = 1
 PE_ORDER = "TPR"
 SQ_LEAD = 2
 G_INTER = (0, 2)
@@ -418,7 +421,7 @@ def tile_rwkv2timemix_pa_t_kernel(tc, x, time_mix, Wr, wkv, sum_k, Wo, out):
             k, h = divmod(i, 2)
             if h == 0:
                 out_tiles[k] = in_pool.tile([P, 2, C_IN], F32, name="o_sb", tag="in")
-            if i >= S_LAST:
+            if i in S_COPIES:
                 nc.scalar.copy(out=out_tiles[k][:, h, :], in_=out_banks[i][:])
             else:
                 nc.vector.tensor_copy(out=out_tiles[k][:, h, :], in_=out_banks[i][:])
@@ -480,7 +483,7 @@ def tile_rwkv2timemix_pa_t_kernel(tc, x, time_mix, Wr, wkv, sum_k, Wo, out):
                 gate(i)
             advance("store", done["project"], store)
             ready = done["quant"]
-            if ready < len(QUANTS) and QUANT_END[ready] <= i - Q_LAG + 1:
+            if ready < len(QUANTS) and QUANT_END[ready] <= i + 1 - (Q_LAG if ready < len(QUANTS) - LAST_Q else LAST_LAG):
                 advance("quant", ready + 1, quantise_gates)
             advance("ratio", N_TILES if done["square"] == N_TILES else done["square"] - D_LAG, ratio)
             if i >= N_TILES:
@@ -489,7 +492,7 @@ def tile_rwkv2timemix_pa_t_kernel(tc, x, time_mix, Wr, wkv, sum_k, Wo, out):
                 if what == "T" and 0 <= i + 1 < N_TILES:
                     turn_ratio(i + 1)
                 if what == "P":
-                    for m in range(1 if i < N_TILES - 2 else 2):
+                    for m in range(1 if i < P2_AT else 2):
                         if done["project"] < N_TILES and QUANT_OF[done["project"]][0] < ready:
                             advance("project", done["project"] + 1, project)
                 if what == "R" and n + 1 < N_TILES:

@@ -125,15 +125,18 @@ def tile_rwkv2timemix_pa_t_kernel(tc, x, time_mix, Wr, wkv, sum_k, Wo, out):
         sumk_tiles[0] = in_pool.tile([P, 2, A_DIM], BF16, name="sumk_t", tag="in")
         first_sumk = pair_rows(sumk_rows, 0)
         nc.sync.dma_start(out=sumk_tiles[0][:, 0, :], in_=first_sumk[:, 0, :])
-        mix_rows = keep.tile([P, P], BF16, name="mix_rows")
+        mix_rows = keep.tile([P, 2 * P], BF16, name="mix_rows")
         nc.vector.memset(mix_rows[:], 0.0)
-        nc.sync.dma_start(out=mix_rows[0:PACK, :], in_=time_mix.rearrange("a b (j p) -> (a b j) p", p=P))
+        nc.sync.dma_start(out=mix_rows[0:2, :], in_=time_mix.rearrange("a b (u k) -> (a b u) k", u=2))
         load_x(0)
         nc.sync.dma_start(out=sumk_tiles[0][:, 1, :], in_=first_sumk[:, 1, :])
-        mix_ps = psum_out.tile([P, P], BF16, name="mix_ps", tag="o_ps")
-        nc.tensor.transpose(mix_ps[:], mix_rows[:], ident_bf[:])
+        mix_ps = psum_out.tile([P, 2, P], BF16, name="mix_ps", tag="o_ps")
+        for e in range(2):
+            nc.tensor.transpose(mix_ps[:, e, :], mix_rows[:, e : 2 * P : 2], ident_bf[:])
         mix_col = keep.tile([P, PACK], F32, name="mix_col")
-        nc.vector.tensor_copy(out=mix_col[:], in_=mix_ps[:, 0:PACK])
+        nc.vector.tensor_copy(
+            out=mix_col[:].rearrange("p (u e) -> p u e", e=2), in_=mix_ps[:, :, 0:2].rearrange("p e u -> p u e")
+        )
         rest_col = keep.tile([P, PACK], F32, name="rest_col")
         nc.vector.tensor_scalar(
             out=rest_col[:], in0=mix_col[:], scalar1=-1.0, scalar2=1.0, op0=ALU.mult, op1=ALU.add
@@ -164,8 +167,9 @@ def tile_rwkv2timemix_pa_t_kernel(tc, x, time_mix, Wr, wkv, sum_k, Wo, out):
                 j = 2 * pair + h
                 for m in range(GROUP_TILES):
                     n = (first + m) % GROUP_TILES
+                    k0 = 2 * P * pair + h
                     nc.tensor.transpose(
-                        x_ps[:, h, P * m : P * (m + 1)], x_tiles[g][:, n, P * j : P * (j + 1)], ident_bf[:]
+                        x_ps[:, h, P * m : P * (m + 1)], x_tiles[g][:, n, k0 : 2 * P * (pair + 1) : 2], ident_bf[:]
                     )
             return x_ps
 
@@ -287,6 +291,21 @@ def tile_rwkv2timemix_pa_t_kernel(tc, x, time_mix, Wr, wkv, sum_k, Wo, out):
                     )
                 if name in W_G and pair % 2 == 0:
                     held["planes"] = ratio_pool.tile([P, PACK, 4 * P], BF16, name="planes_w", tag="ratio", align_bytes=64)
+                if passes == 1:
+                    word_ps = psum_turn.tile([P, 2, 2, P], F32, name="word_ps", tag="turn")
+                    for h in range(2):
+                        c, m = units[2 * pair + h]
+                        rows = halves[m // (row_tiles // 2)][:, m % (row_tiles // 2), :].bitcast(F32)
+                        for u in range(2):
+                            nc.tensor.transpose(word_ps[:, u, h, :], rows[:, P * u : P * (u + 1)], ident_f32[:])
+                    nc.vector.tensor_copy(
+                        out=held["grouped"][:, 2 * P * pair : 2 * P * (pair + 1), :]
+                        .rearrange("p r j -> p (r j)")
+                        .bitcast(F32)
+                        .rearrange("p (b i u) -> p b u i", i=4, u=2),
+                        in_=word_ps[:].rearrange("p u h (b i) -> p (h b) u i", i=4),
+                    )
+                    return
                 w_ps = psum_turn.tile([P, PACK, 2, P], BF16, name="w_ps", tag="turn")
                 for h in range(2):
                     c, m = units[2 * pair + h]

@@ -33,12 +33,12 @@ PR = 4
 PO = 2
 SQ0 = 4
 A1 = 9
-REST = 5
+REST = 0
 STAGE_G = 5
 WO_AT = 20
 WR_AT = 5
 X_AT = 2
-X_STEP = 4
+X_STEP = 3
 W_G = ()
 WR_POS = 2
 WO_POS = 7
@@ -54,8 +54,10 @@ SQ_MORE = 0
 G_SQ = ()
 D_LAG = 1
 Q_LAG = 2
-S_COPIES = range(22, 31)
+S_COPIES = [*range(22, 29), 30]
 P2_AT = 28
+FREE_FROM = 28
+LAST_PAIRS = 14
 LAST_Q = 1
 LAST_LAG = 1
 PE_ORDER = "TPR"
@@ -424,7 +426,10 @@ def tile_rwkv2timemix_pa_t_kernel(tc, x, time_mix, Wr, wkv, sum_k, Wo, out):
 
         def project(i):
             k, h = QUANT_OF[i]
-            out_banks[i] = psum_out.tile([P, C_IN], F32, name="o_ps", tag="o_ps")
+            if i < FREE_FROM:
+                out_banks[i] = psum_out.tile([P, C_IN], F32, name="o_ps", tag="o_ps")
+            else:
+                out_banks[i] = psum_turn.tile([P, C_IN], F32, name="o_ps", tag="turn")
             for c in range(A_PASSES):
                 nc.tensor.matmul_mx(
                     out=out_banks[i][:],
@@ -445,7 +450,7 @@ def tile_rwkv2timemix_pa_t_kernel(tc, x, time_mix, Wr, wkv, sum_k, Wo, out):
             else:
                 nc.vector.tensor_copy(out=out_tiles[k][:, h, :], in_=out_banks[i][:])
             dst = pair_rows(out_rows, k)
-            if k == N_TILES // 2 - 1:
+            if k >= LAST_PAIRS:
                 nc.sync.dma_start(out=dst[:, h, :], in_=out_tiles[k][:, h, :])
             elif h == 1:
                 nc.sync.dma_start(out=dst, in_=out_tiles[k][:])
@@ -511,7 +516,7 @@ def tile_rwkv2timemix_pa_t_kernel(tc, x, time_mix, Wr, wkv, sum_k, Wo, out):
                 if what == "T" and 0 <= i + 1 < N_TILES:
                     turn_ratio(i + 1)
                 if what == "P":
-                    for m in range(1 if i < P2_AT else 2):
+                    for m in range(1 if i < P2_AT else 2 if i < N_TILES else 4):
                         if done["project"] < N_TILES and QUANT_OF[done["project"]][0] < ready:
                             advance("project", done["project"] + 1, project)
                 if what == "R" and n + 1 < N_TILES:

from contextlib import ExitStack

import concourse.mybir as mybir
from concourse.masks import make_identity

FLOPS = 2 * 4096 * 512 * 1024 * 2

BF16 = mybir.dt.bfloat16
F32 = mybir.dt.float32
U32 = mybir.dt.uint32
U8 = mybir.dt.uint8
FP8X4 = mybir.dt.float8_e4m3fn_x4
ACT = mybir.ActivationFunctionType
ALU = mybir.AluOpType

P = 128
PACK = 4
K_PASS = P * PACK
N_SEQ, SEQ_LEN, C_IN, A_DIM = 4, 1024, 512, 1024
A_PASSES = A_DIM // K_PASS
A_BLOCKS = A_DIM // P
N_TILES = N_SEQ * SEQ_LEN // P
GROUP = 512
GROUP_TILES = GROUP // P
N_GROUPS = N_TILES // GROUP_TILES
PAD = 2
W_AHEAD = 6
IN_BUFS = 4
WB = 3
BIG = 7
PA = 2
PR = 4
PO = 2
SQ0 = 4
A1 = 9
REST = 0
STAGE_G = 5
WO_AT = 20
WR_AT = 5
X_AT = 2
X_STEP = 3
W_G = ()
WR_POS = 2
WO_POS = 7
REST_RATE = 3
W_LEAD = 2
W_EARLY = 4
PREP_T = 30
R0_AT = 25
MGROUPS = (1, 3, 4, 5, 6, 7)
E_LAG = 2
SQ_TICKS = (0, 1, 3)
SQ_MORE = 0
G_SQ = ()
D_LAG = 1
Q_LAG = 2
S_COPIES = [*range(22, 29), 30]
P2_AT = 28
FREE_FROM = 28
LAST_PAIRS = 14
LAST_Q = 1
LAST_LAG = 1
PE_ORDER = "TPR"
SQ_LEAD = 2
G_INTER = (0, 2)
QUANTS = [4] * 7 + [2, 2]
QUANT_OF = [(k, h) for k in range(len(QUANTS)) for h in range(QUANTS[k])]
QUANT_END = [sum(QUANTS[: k + 1]) for k in range(len(QUANTS))]


def tile_rwkv2timemix_pa_t_kernel(tc, x, time_mix, Wr, wkv, sum_k, Wo, out):
    nc = tc.nc
    x_rows = x.flatten_outer_dims()
    wkv_rows = wkv.flatten_outer_dims()
    sumk_rows = sum_k.flatten_outer_dims()
    out_rows = out.flatten_outer_dims()

    with ExitStack() as ctx:
        keep = ctx.enter_context(tc.tile_pool(name="keep", bufs=1))
        big_pool = ctx.enter_context(tc.tile_pool(name="big_pool", bufs=BIG))
        xq_pool = ctx.enter_context(tc.tile_pool(name="xq_pool", bufs=N_SEQ))
        in_pool = ctx.enter_context(tc.tile_pool(name="in_pool", bufs=IN_BUFS))
        w_pool = ctx.enter_context(tc.tile_pool(name="w_pool", bufs=WB))
        ratio_pool = ctx.enter_context(tc.tile_pool(name="ratio_pool", bufs=N_TILES))
        gate_pool = ctx.enter_context(tc.tile_pool(name="gate_pool", bufs=2))
        gq_pool = ctx.enter_context(tc.tile_pool(name="gq_pool", bufs=2))
        psum_r = ctx.enter_context(tc.psum_pool(name="psum_r", bufs=PA))
        psum_turn = ctx.enter_context(tc.psum_pool(name="psum_turn", bufs=PR))
        psum_out = ctx.enter_context(tc.psum_pool(name="psum_out", bufs=PO))
        ctx.enter_context(tc.manual_schedule())

        sumk_tiles, wkv_tiles, ratio_tiles, x_tiles, xts, grouped = {}, {}, {}, {}, {}, {}
        x_words, x_scales, tanh_tiles, r_banks, ratio_banks = {}, {}, {}, {}, {}
        gate_tiles, gate_words, gate_scales, out_banks, out_tiles = {}, {}, {}, {}, {}

        def pair_rows(rows, k):
            g, h = divmod(k, 2)
            group = rows[GROUP * g : GROUP * (g + 1), :].rearrange("(p n) w -> p n w", n=GROUP_TILES)
            return group[:, 2 * h : 2 * h + 2, :]

        def load_sumk(k):
            sumk_tiles[k] = in_pool.tile([P, 2, A_DIM], BF16, name="sumk_t", tag="in")
            nc.sync.dma_start(out=sumk_tiles[k][:], in_=pair_rows(sumk_rows, k))

        def load_wkv(k):
            wkv_tiles[k] = w_pool.tile([P, 2, A_DIM], BF16, name="wkv_t")
            nc.sync.dma_start(out=wkv_tiles[k][:], in_=pair_rows(wkv_rows, k))

        def load_rows(dst, rows):
            nc.sync.dma_start(out=dst, in_=rows.rearrange("(n p) w -> p n w", p=P))

        def stage(g, shape, dtype, name):
            if g < STAGE_G:
                return ratio_pool.tile(shape, dtype, name=name, tag="ratio", align_bytes=64)
            return big_pool.tile(shape, dtype, name=name, tag="big", align_bytes=64)

        def load_x(g):
            x_tiles[g] = stage(g, [P, GROUP_TILES, C_IN], BF16, "x_t")
            rows = x_rows[GROUP * g : GROUP * (g + 1), :].rearrange("(p n) w -> p n w", n=GROUP_TILES)
            nc.sync.dma_start(out=x_tiles[g][:], in_=rows)

        ident_bf = keep.tile([P, P], BF16, name="ident_bf")
        make_identity(nc, ident_bf[:])
        ident_f32 = keep.tile([P, P], F32, name="ident_f32")
        make_identity(nc, ident_f32[:])

        sumk_tiles[0] = in_pool.tile([P, 2, A_DIM], BF16, name="sumk_t", tag="in")
        first_sumk = pair_rows(sumk_rows, 0)
        nc.sync.dma_start(out=sumk_tiles[0][:, 0, :], in_=first_sumk[:, 0, :])
        mix_rows = keep.tile([P, 2 * P], BF16, name="mix_rows")
        nc.vector.memset(mix_rows[:], 0.0)
        nc.sync.dma_start(out=mix_rows[0:2, :], in_=time_mix.rearrange("a b (u k) -> (a b u) k", u=2))
        load_x(0)
        nc.sync.dma_start(out=sumk_tiles[0][:, 1, :], in_=first_sumk[:, 1, :])
        mix_ps = psum_out.tile([P, 2, P], BF16, name="mix_ps", tag="o_ps")
        for e in range(2):
            nc.tensor.transpose(mix_ps[:, e, :], mix_rows[:, e : 2 * P : 2], ident_bf[:])
        mix_col = keep.tile([P, PACK], F32, name="mix_col")
        nc.vector.tensor_copy(
            out=mix_col[:].rearrange("p (u e) -> p u e", e=2), in_=mix_ps[:, :, 0:2].rearrange("p e u -> p u e")
        )
        rest_col = keep.tile([P, PACK], F32, name="rest_col")
        nc.vector.tensor_scalar(
            out=rest_col[:], in0=mix_col[:], scalar1=-1.0, scalar2=1.0, op0=ALU.mult, op1=ALU.add
        )
        diags = keep.tile([P, 2, PACK, P], BF16, name="diags")
        for j in range(PACK):
            for h in range(2):
                nc.vector.tensor_scalar(
                    out=diags[:, h, j, :],
                    in0=ident_bf[:],
                    scalar1=mix_col[:, j : j + 1],
                    scalar2=1.0 - 2.0 * h,
                    op0=ALU.mult,
                    op1=ALU.mult,
                )

        wr_words = keep.tile([P, A_DIM], U32, name="wr_words", align_bytes=64)
        wr_scales = keep.tile([P, A_DIM], U8, name="wr_scales", align_bytes=64)
        wo_words = keep.tile([P, A_PASSES, C_IN], U32, name="wo_words", align_bytes=64)
        wo_scales = keep.tile([P, A_PASSES, C_IN], U8, name="wo_scales", align_bytes=64)

        def new_xt(g):
            xts[g] = big_pool.tile([P, PACK, GROUP + PAD], BF16, name="xt", tag="big", align_bytes=64)

        def turn_x(g, pair, first):
            x_ps = psum_turn.tile([P, 2, GROUP], BF16, name="x_ps", tag="turn")
            for h in range(2):
                j = 2 * pair + h
                for m in range(GROUP_TILES):
                    n = (first + m) % GROUP_TILES
                    k0 = 2 * P * pair + h
                    nc.tensor.transpose(
                        x_ps[:, h, P * m : P * (m + 1)], x_tiles[g][:, n, k0 : 2 * P * (pair + 1) : 2], ident_bf[:]
                    )
            return x_ps

        def group_half(g):
            s, h = divmod(g, 2)
            if s not in grouped:
                grouped[s] = gate_pool.tile([P, SEQ_LEN, PACK], BF16, name="grouped_t", tag="gate", align_bytes=64)
            return grouped[s][:, GROUP * h : GROUP * (h + 1), :]

        def carry_last(g, pair, x_ps, end):
            if g % 2 == 0:
                nc.vector.tensor_copy(
                    out=xts[g + 1][:, 2 * pair : 2 * pair + 2, 0:PAD], in_=x_ps[:, :, end - PAD : end]
                )

        def x_turn(g):
            if g % 2 == 0:
                new_xt(g)
                nc.vector.memset(xts[g][:, :, 0:PAD], 0.0)
                new_xt(g + 1)
            for pair in range(2):
                x_ps = turn_x(g, pair, GROUP_TILES - 1)
                nc.vector.tensor_copy(out=xts[g][:, 2 * pair : 2 * pair + 2, PAD : PAD + GROUP], in_=x_ps[:])
                carry_last(g, pair, x_ps, P)

        def x_mix(g, n):
            a = PAD + P * ((n + 1) % GROUP_TILES)
            b = PAD + P * n - (1 if n == 0 else 0)
            now = xts[g][:, :, a : a + P]
            before = xts[g][:, :, b : b + P]
            m_ps = psum_out.tile([P, PACK, P], F32, name="m_ps", tag="o_ps")
            for j in range(PACK):
                nc.tensor.matmul(m_ps[:, j, :], lhsT=diags[:, 0, j, :], rhs=now[:, j, :], start=True, stop=False)
                nc.tensor.matmul(m_ps[:, j, :], lhsT=diags[:, 1, j, :], rhs=before[:, j, :], start=False, stop=True)
            nc.vector.tensor_tensor(
                out=group_half(g)[:, P * n : P * (n + 1), :].rearrange("p (b i) j -> p b j i", i=4),
                in0=m_ps[:].rearrange("p j (b i) -> p b j i", i=4),
                in1=before.rearrange("p j (b i) -> p b j i", i=4),
                op=ALU.add,
            )

        def direct_jobs(g):
            held = {}

            def carry(pair):
                if pair == 0:
                    new_xt(g + 1)
                    held["planes"] = stage(g, [P, PACK, GROUP], BF16, "planes")
                held["carry"] = ratio_pool.tile([P, 2, GROUP], F32, name="carry_t", tag="ratio", align_bytes=64)
                nc.vector.memset(held["carry"][:, :, 0:1], 0.0)
                held[pair] = turn_x(g, pair, 0)
                for h in range(2):
                    j = 2 * pair + h
                    for dst, src in ((slice(1, P), slice(GROUP - P, GROUP - 1)), (slice(P, GROUP), slice(0, GROUP - P))):
                        nc.vector.tensor_scalar_mul(
                            out=held["carry"][:, h, dst], in0=held[pair][:, h, src], scalar1=rest_col[:, j : j + 1]
                        )
                carry_last(g, pair, held[pair], GROUP)

            def mix(pair):
                for h in range(2):
                    j = 2 * pair + h
                    nc.vector.scalar_tensor_tensor(
                        out=held["planes"][:, j, :],
                        in0=held[pair][:, h, :],
                        scalar=mix_col[:, j : j + 1],
                        in1=held["carry"][:, h, :],
                        op0=ALU.mult,
                        op1=ALU.add,
                    )

            def interleave():
                planes = held["planes"][:].rearrange("p j t -> p t j")
                if g in G_INTER:
                    nc.gpsimd.tensor_scalar(
                        out=group_half(g), in0=planes, scalar1=1.0, scalar2=0.0, op0=ALU.mult, op1=ALU.add
                    )
                else:
                    nc.vector.tensor_copy(out=group_half(g), in_=planes)

            return [lambda: carry(0), lambda: mix(0), lambda: carry(1), lambda: mix(1), interleave]

        def x_quant(s):
            x_words[s] = xq_pool.tile([P, SEQ_LEN], U32, name="x_words_t", align_bytes=64)
            x_scales[s] = xq_pool.tile([P, SEQ_LEN], U8, name="x_scales_t", align_bytes=64)
            nc.vector.quantize_mx(
                out=x_words[s][:].bitcast(FP8X4),
                scales=x_scales[s][:],
                in_=grouped[s][:].rearrange("p t j -> p (t j)"),
            )

        def x_jobs(g):
            if g in MGROUPS:
                return [lambda: x_turn(g)] + [lambda n=n: x_mix(g, n) for n in range(GROUP_TILES)]
            return direct_jobs(g)

        def weight_loads(w, row_tiles, width):
            half_tiles = row_tiles // 2
            step = 2 * P * C_IN // width // P
            halves = {}

            def load(h, s):
                if s == 0:
                    pool, tag = (ratio_pool, "ratio") if width == C_IN else (big_pool, "big")
                    halves[h] = pool.tile([P, half_tiles, width], BF16, name="w_t", tag=tag, align_bytes=64)
                r0 = P * (half_tiles * h + s)
                load_rows(halves[h][:, s : s + step, :], w[r0 : r0 + P * step, :])

            return halves, [lambda h=h, s=s: load(h, s) for h in range(2) for s in range(0, half_tiles, step)]

        def weight_jobs(name, halves, row_tiles, passes, words, scales):
            units = [(c, m) for c in range(passes) for m in range(row_tiles)]
            held = {}

            def turn(pair):
                if pair == 0:
                    held["grouped"] = gate_pool.tile(
                        [P, len(units) * P, PACK], BF16, name="grouped_w", tag="gate", align_bytes=64
                    )
                if name in W_G and pair % 2 == 0:
                    held["planes"] = ratio_pool.tile([P, PACK, 4 * P], BF16, name="planes_w", tag="ratio", align_bytes=64)
                if passes == 1:
                    word_ps = psum_turn.tile([P, 2, 2, P], F32, name="word_ps", tag="turn")
                    for h in range(2):
                        c, m = units[2 * pair + h]
                        rows = halves[m // (row_tiles // 2)][:, m % (row_tiles // 2), :].bitcast(F32)
                        for u in range(2):
                            nc.tensor.transpose(word_ps[:, u, h, :], rows[:, P * u : P * (u + 1)], ident_f32[:])
                    nc.vector.tensor_copy(
                        out=held["grouped"][:, 2 * P * pair : 2 * P * (pair + 1), :]
                        .rearrange("p r j -> p (r j)")
                        .bitcast(F32)
                        .rearrange("p (b i u) -> p b u i", i=4, u=2),
                        in_=word_ps[:].rearrange("p u h (b i) -> p (h b) u i", i=4),
                    )
                    return
                w_ps = psum_turn.tile([P, PACK, 2, P], BF16, name="w_ps", tag="turn")
                for h in range(2):
                    c, m = units[2 * pair + h]
                    w_t = halves[m // (row_tiles // 2)]
                    for j in range(PACK):
                        k0 = K_PASS * c + P * j
                        nc.tensor.transpose(w_ps[:, j, h, :], w_t[:, m % (row_tiles // 2), k0 : k0 + P], ident_bf[:])
                if name not in W_G:
                    nc.vector.tensor_copy(
                        out=held["grouped"][:, 2 * P * pair : 2 * P * (pair + 1), :].rearrange(
                            "p (b i) j -> p b j i", i=4
                        ),
                        in_=w_ps[:].rearrange("p j h (b i) -> p (h b) j i", i=4),
                    )
                    return
                nc.vector.tensor_copy(
                    out=held["planes"][:, :, 2 * P * (pair % 2) : 2 * P * (pair % 2 + 1)],
                    in_=w_ps[:].rearrange("p j h r -> p j (h r)"),
                )
                if pair % 2 == 1:
                    nc.gpsimd.tensor_scalar(
                        out=held["grouped"][:, 4 * P * (pair // 2) : 4 * P * (pair // 2 + 1), :],
                        in0=held["planes"][:].rearrange("p j r -> p r j"),
                        scalar1=1.0,
                        scalar2=0.0,
                        op0=ALU.mult,
                        op1=ALU.add,
                    )

            def quant():
                nc.vector.quantize_mx(
                    out=words.bitcast(FP8X4), scales=scales, in_=held["grouped"][:].rearrange("p r j -> p (r j)")
                )

            return [lambda q=q: turn(q) for q in range(len(units) // 2)] + [quant]

        def root(i):
            ratio_tiles[i] = ratio_pool.tile([P, A_DIM], F32, name="ratio_t", tag="ratio", align_bytes=64)
            nc.scalar.activation(
                out=ratio_tiles[i][:], in_=sumk_tiles[i // 2][:, i % 2, :], func=ACT.Abs_reciprocal_sqrt
            )

        def square(i):
            if i in G_SQ:
                nc.gpsimd.tensor_tensor(
                    out=ratio_tiles[i][:], in0=ratio_tiles[i][:], in1=ratio_tiles[i][:], op=ALU.mult
                )
                return
            nc.scalar.activation(out=ratio_tiles[i][:], in_=ratio_tiles[i][:], func=ACT.Square)

        def ratio(i):
            nc.gpsimd.tensor_tensor(
                out=ratio_tiles[i][:], in0=wkv_tiles[i // 2][:, i % 2, :], in1=ratio_tiles[i][:], op=ALU.mult
            )

        def receptance(u):
            k, c = divmod(u, A_PASSES)
            g, part = divmod(k, N_TILES // N_SEQ // 2)
            t0 = 2 * P * part
            for b in range(2):
                r_banks[u, b] = psum_r.tile([P, 2, 2 * P], F32, name="r_ps")
                for h in range(2):
                    a0 = K_PASS * c + P * (2 * b + h)
                    nc.tensor.matmul_mx(
                        out=r_banks[u, b][:, h, :],
                        lhsT=wr_words[:, a0 : a0 + P].bitcast(FP8X4),
                        lhsT_scale=wr_scales[:, a0 : a0 + P],
                        rhs=x_words[g][:, t0 : t0 + 2 * P].bitcast(FP8X4),
                        rhs_scale=x_scales[g][:, t0 : t0 + 2 * P],
                        start=True,
                        stop=True,
                    )

        def tanh(u):
            tanh_tiles[u] = big_pool.tile([P, PACK, 2 * P], F32, name="tanh_t", tag="big", align_bytes=64)
            for b in range(2):
                nc.scalar.activation(
                    out=tanh_tiles[u][:, 2 * b : 2 * b + 2, :], in_=r_banks[u, b][:], func=ACT.Sigmoid
                )

        def turn_ratio(u):
            k, c = divmod(u, A_PASSES)
            for h in range(2):
                ratio_banks[u, h] = psum_turn.tile([P, PACK, P], F32, name="ratio_ps", tag="turn")
                for j in range(PACK):
                    a0 = K_PASS * c + P * j
                    nc.tensor.transpose(
                        ratio_banks[u, h][:, j, :], ratio_tiles[2 * k + h][:, a0 : a0 + P], ident_f32[:]
                    )

        def gate(u):
            k, c = divmod(u, A_PASSES)
            for h in range(2):
                q, m = QUANT_OF[2 * k + h]
                if c == 0 and m == 0:
                    gate_tiles[q] = gate_pool.tile(
                        [P, QUANTS[q], A_PASSES, P, PACK], BF16, name="gate_t", tag="gate", align_bytes=64
                    )
                nc.vector.tensor_tensor(
                    out=gate_tiles[q][:, m, c, :, :].rearrange("p (b i) j -> p b j i", i=4),
                    in0=tanh_tiles[u][:, :, P * h : P * (h + 1)].rearrange("p j (b i) -> p b j i", i=4),
                    in1=ratio_banks[u, h][:].rearrange("p j (b i) -> p b j i", i=4),
                    op=ALU.mult,
                )

        def quantise_gates(k):
            gate_words[k] = big_pool.tile(
                [P, QUANTS[k], A_PASSES, P], U32, name="gate_words_t", tag="big", align_bytes=64
            )
            gate_scales[k] = gq_pool.tile([P, QUANTS[k], A_PASSES, P], U8, name="gate_scales_t", align_bytes=64)
            nc.vector.quantize_mx(
                out=gate_words[k][:].rearrange("p q c t -> p (q c t)").bitcast(FP8X4),
                scales=gate_scales[k][:].rearrange("p q c t -> p (q c t)"),
                in_=gate_tiles[k][:].rearrange("p q c t j -> p (q c t j)"),
            )

        def project(i):
            k, h = QUANT_OF[i]
            if i < FREE_FROM:
                out_banks[i] = psum_out.tile([P, C_IN], F32, name="o_ps", tag="o_ps")
            else:
                out_banks[i] = psum_turn.tile([P, C_IN], F32, name="o_ps", tag="turn")
            for c in range(A_PASSES):
                nc.tensor.matmul_mx(
                    out=out_banks[i][:],
                    lhsT=gate_words[k][:, h, c, :].bitcast(FP8X4),
                    lhsT_scale=gate_scales[k][:, h, c, :],
                    rhs=wo_words[:, c, :].bitcast(FP8X4),
                    rhs_scale=wo_scales[:, c, :],
                    start=(c == 0),
                    stop=(c == A_PASSES - 1),
                )

        def store(i):
            k, h = divmod(i, 2)
            if h == 0:
                out_tiles[k] = in_pool.tile([P, 2, C_IN], F32, name="o_sb", tag="in")
            if i in S_COPIES:
                nc.scalar.copy(out=out_tiles[k][:, h, :], in_=out_banks[i][:])
            else:
                nc.vector.tensor_copy(out=out_tiles[k][:, h, :], in_=out_banks[i][:])
            dst = pair_rows(out_rows, k)
            if k >= LAST_PAIRS:
                nc.sync.dma_start(out=dst[:, h, :], in_=out_tiles[k][:, h, :])
            elif h == 1:
                nc.sync.dma_start(out=dst, in_=out_tiles[k][:])

        wr_halves, wr_loads = weight_loads(Wr, A_DIM // P, C_IN)
        wo_halves, wo_loads = weight_loads(Wo, C_IN // P, A_DIM)
        load_sumk(1)
        load_x(1)
        load_sumk(2)
        side_loads = {WO_AT + q: wo_loads[q : q + 1] for q in range(4)}
        for q in range(4):
            side_loads.setdefault(WR_AT + q, []).append(wr_loads[q])
        for g in range(2, N_GROUPS):
            side_loads.setdefault(X_AT + X_STEP * (g - 2), []).append(lambda g=g: load_x(g))

        xj = [x_jobs(g) for g in range(N_GROUPS)]
        wr = weight_jobs("wr", wr_halves, A_DIM // P, 1, wr_words[:], wr_scales[:])
        wo = weight_jobs(
            "wo",
            wo_halves,
            C_IN // P,
            A_PASSES,
            wo_words[:].rearrange("p c r -> p (c r)"),
            wo_scales[:].rearrange("p c r -> p (c r)"),
        )
        jobs = JOBS(xj, wr, wo, [lambda s=s: x_quant(s) for s in range(N_SEQ)])

        done = {"jobs": 0, "square": 0, "ratio": 0, "wkv": 0, "quant": 0, "project": 0, "store": 0}

        def advance(what, upto, act):
            while done[what] < upto:
                act(done[what])
                done[what] += 1

        for n in range(N_TILES):
            root(n)
            if n % 2 == 1 and n // 2 + 3 < N_TILES // 2:
                load_sumk(n // 2 + 3)
            for load in side_loads.get(n, []):
                load()
            advance("wkv", min(A1 + W_LEAD, (n + 1 - SQ0 + W_EARLY) * A1 // (N_TILES - SQ0) + 1) // 2, load_wkv)
            advance("square", min(A1, 2 * done["wkv"], (n + 1 - SQ0) * A1 // (N_TILES - SQ0)), square)
            advance("ratio", done["square"], ratio)
            advance("jobs", min(len(jobs) - REST, (n + 1) * (len(jobs) - REST) // PREP_T), lambda q: jobs[q]())
            if n == R0_AT:
                receptance(0)

        for n in range(N_TILES + 20):
            i = n - E_LAG
            if n < N_TILES:
                tanh(n)
            advance("jobs", min(len(jobs), len(jobs) - REST + (n + 1) * REST_RATE), lambda q: jobs[q]())
            if 0 <= i < N_TILES:
                gate(i)
            advance("store", done["project"], store)
            ready = done["quant"]
            if ready < len(QUANTS) and QUANT_END[ready] <= i + 1 - (Q_LAG if ready < len(QUANTS) - LAST_Q else LAST_LAG):
                advance("quant", ready + 1, quantise_gates)
            advance("ratio", N_TILES if done["square"] == N_TILES else done["square"] - D_LAG, ratio)
            if i >= N_TILES:
                ready = done["quant"]
            for what in PE_ORDER:
                if what == "T" and 0 <= i + 1 < N_TILES:
                    turn_ratio(i + 1)
                if what == "P":
                    for m in range(1 if i < P2_AT else 2 if i < N_TILES else 4):
                        if done["project"] < N_TILES and QUANT_OF[done["project"]][0] < ready:
                            advance("project", done["project"] + 1, project)
                if what == "R" and n + 1 < N_TILES:
                    receptance(n + 1)
            advance("wkv", min(N_TILES, done["ratio"] + W_AHEAD) // 2, load_wkv)
            advance("square", min(N_TILES, A1 + SQ_MORE + sum(1 for m in range(n + 1) if m % 4 in SQ_TICKS)), square)


def JOBS(xj, wr, wo, quants):
    jobs = []
    waiting = []
    for g in range(N_GROUPS):
        body = xj[g][1:] if g > 0 else xj[g]
        nxt = xj[g + 1][:1] if g + 1 < N_GROUPS else []
        jobs += body[:2] + waiting + body[2:3] + nxt + body[3:]
        waiting = quants[g // 2 : g // 2 + 1] if g % 2 == 1 else []
        if g == WR_POS:
            jobs += wr[:4]
            waiting = waiting + wr[4:]
    jobs += waiting + wo
    return jobs
